import numpy as np
import ml_dtypes


def mxq(x, axis, fmt="e4m3"):
    dtype, down = {"e4m3": (ml_dtypes.float8_e4m3fn, 7), "e5m2": (ml_dtypes.float8_e5m2, 14)}[fmt]
    v = np.moveaxis(np.asarray(x, np.float32).astype(ml_dtypes.bfloat16).astype(np.float64), axis, -1)
    blocks = v.reshape(v.shape[:-1] + (-1, 32))
    amax = np.abs(blocks).max(-1, keepdims=True)
    byte = np.maximum(np.where(amax > 0, np.frexp(amax)[1] - 1 + 127, 0) - down, 1)
    scale = np.exp2(byte - 127.0)
    codes = (blocks / scale).astype(np.float32).astype(dtype).astype(np.float64)
    return np.moveaxis((codes * scale).reshape(v.shape), -1, axis)


WIDE = False


def mx_kscale(k):
    if not WIDE:
        return np.ones(k)
    levels = np.array([10, -10, 5, -5, 0])
    a = np.random.permutation(np.resize(levels, k // 512 * 4)).reshape(k // 512, 4)
    idx = np.arange(k)
    return np.exp2(a[idx // 512, idx % 128 // 32])


BF16 = ml_dtypes.bfloat16


def bf(x):
    return np.asarray(x, np.float32).astype(BF16)


def f64(x):
    return np.asarray(x).astype(np.float64)


E2M1 = np.array([0.0, 0.5, 1.0, 1.5, 2.0, 3.0, 4.0, 6.0, -0.0, -0.5, -1.0, -1.5, -2.0, -3.0, -4.0, -6.0])


def pack_weight(w, fmt):
    k, n = w.shape
    w = f64(bf(w)).reshape(k // 32, 32, n)
    amax = np.abs(w).max(1)
    if fmt == "e4m3":
        byte = np.frexp(amax)[1] - 1 + 127 - 7
    else:
        mant, ex = np.frexp(amax / 6.0)
        byte = np.where(mant > 0.5, ex, ex - 1) + 127
    byte = np.clip(np.where(amax > 0, byte, 1), 1, 254)
    scaled = (w * np.exp2(127.0 - byte)[:, None, :]).reshape(k, n).astype(np.float32)
    by_word = np.ascontiguousarray(scaled.reshape(k // 512, 128, 4, n).transpose(0, 1, 3, 2))
    if fmt == "e4m3":
        words = by_word.astype(ml_dtypes.float8_e4m3fn).view(np.uint8)
    else:
        c = by_word.astype(ml_dtypes.float4_e2m1fn).view(np.uint8) & 0xF
        words = c[..., 0::2] | (c[..., 1::2] << 4)
    return np.ascontiguousarray(words), np.ascontiguousarray(byte.astype(np.uint8).reshape(k // 512, 16, n))


def unpack_weight(words, scales, fmt):
    g, p, n, _ = words.shape
    if fmt == "e4m3":
        vals = np.ascontiguousarray(words).view(ml_dtypes.float8_e4m3fn).astype(np.float64)
    else:
        nib = np.empty((g, p, n, 4), np.uint8)
        nib[..., 0::2] = words & 0xF
        nib[..., 1::2] = words >> 4
        vals = E2M1[nib]
    vals = vals * np.repeat(np.exp2(scales.astype(np.float64) - 127.0), 8, axis=1)[..., None]
    return vals.transpose(0, 1, 3, 2).reshape(g * 512, n)


NQ, NK, QS, KS, F, DEG = 1024, 1024, 512, 512, 512, 32
EPS = 1e-5
SLOPE = 0.01
FMT = "e4m3"


def leaky(v):
    return np.where(v >= 0, v, SLOPE * v)


def setup_inputs():
    s, t = mx_kscale(QS), mx_kscale(F)
    x = bf(np.random.standard_normal((NQ, QS)) * s)
    w1_words, w1_scales = pack_weight(np.random.standard_normal((QS, F)) / np.sqrt(QS) / s[:, None] * t, FMT)
    b1 = bf(np.random.standard_normal(F) * 0.5 * t)
    w2_words, w2_scales = pack_weight(np.random.standard_normal((F, F)) / np.sqrt(F) / t[:, None], FMT)
    b2 = bf(np.random.standard_normal(F) * 0.5)
    gamma = bf(1.0 + 0.1 * np.random.standard_normal(F))
    beta = bf(0.1 * np.random.standard_normal(F))
    return {"x": x,
            "w1_words": w1_words,
            "w1_scales": w1_scales,
            "b1": b1,
            "w2_words": w2_words,
            "w2_scales": w2_scales,
            "b2": b2,
            "gamma": gamma,
            "beta": beta}


def reference(x, w1_words, w1_scales, b1, w2_words, w2_scales, b2, gamma, beta):
    h = leaky((mxq(f64(x), 1, "e4m3") @ unpack_weight(w1_words, w1_scales, FMT)) + f64(b1))
    h = leaky((mxq(h, 1, "e4m3") @ unpack_weight(w2_words, w2_scales, FMT)) + f64(b2))
    mean = h.mean(axis=0)
    var = h.var(axis=0)
    return f64(gamma) * (h - mean) / np.sqrt(var + EPS) + f64(beta)

@@ -1,0 +1,293 @@
+from contextlib import ExitStack
+
+import concourse.mybir as mybir
+from concourse.masks import make_identity
+
+F32 = mybir.dt.float32
+BF16 = mybir.dt.bfloat16
+I32 = mybir.dt.int32
+U32 = mybir.dt.uint32
+U8 = mybir.dt.uint8
+FP8X4 = mybir.dt.float8_e4m3fn_x4
+ALU = mybir.AluOpType
+ACT = mybir.ActivationFunctionType
+
+P = 128
+PACK = 4
+ROWS = 1024
+FEAT = 512
+ROW_TILES = ROWS // P
+FEAT_TILES = FEAT // P
+PAIRS = ROW_TILES // 2
+HALVES = 2
+HALF = ROWS // HALVES
+WORDS = FEAT // 2
+EPS = 1e-5
+SLOPE = 0.01
+
+FLOPS = 2 * 2 * ROWS * FEAT * FEAT
+
+
+def tile_attention_prop_pa_kernel(
+    tc, x, w1_words, w1_scales, b1, w2_words, w2_scales, b2, gamma, beta, out
+):
+    nc = tc.nc
+    with ExitStack() as ctx:
+        ctx.enter_context(tc.manual_schedule())
+        keep = ctx.enter_context(tc.tile_pool(name="keep", bufs=1))
+        work = ctx.enter_context(tc.tile_pool(name="work", bufs=3))
+        psum = ctx.enter_context(tc.psum_pool(name="psum", bufs=8))
+
+        x_sb = keep.tile([P, ROW_TILES, FEAT], BF16)
+        w_bytes = keep.tile([P, 2, PACK * FEAT], U8, align_bytes=64)
+        w_planes = keep.tile([P, 2, FEAT], U8, align_bytes=64)
+        ones = keep.tile([P, P], BF16)
+        b1_row = keep.tile([P, FEAT], BF16)
+        vec_rows = keep.tile([P, P], BF16)
+        ident = keep.tile([P, P], F32)
+        ident_bf = keep.tile([P, P], BF16)
+        x_codes = keep.tile([P, ROWS], U32, align_bytes=64)
+        x_plane = keep.tile([P, ROWS], U8, align_bytes=64)
+        h_codes = keep.tile([P, ROWS], U32, align_bytes=64)
+        h_plane = keep.tile([P, ROWS], U8, align_bytes=64)
+        h2 = keep.tile([P, FEAT_TILES, ROWS], F32)
+        sums = keep.tile([P, FEAT_TILES, HALVES], F32)
+        stats = keep.tile([P, FEAT_TILES, 8], F32)
+        out_sb = keep.tile([P, ROW_TILES, FEAT], F32)
+
+        nc.vector.memset(w_planes[:].rearrange("p w n -> p (w n)").bitcast(I32), 0)
+        nc.vector.memset(b1_row[:], 0.0)
+        nc.vector.memset(ones[:], 1.0)
+        nc.vector.memset(vec_rows[:], 0.0)
+        make_identity(nc, ident[:])
+        nc.vector.tensor_copy(out=ident_bf[:], in_=ident[:])
+        warm = keep.tile([P, 1], F32)
+        nc.scalar.activation(out=warm[:], in_=ones[:, 0:1], func=ACT.Sqrt)
+
+        x_rows = x.rearrange("(p i) k -> p i k", i=ROW_TILES)
+        out_rows = out.rearrange("(p i) f -> p i f", i=ROW_TILES)
+
+        def load_x(g):
+            nc.sync.dma_start(out=x_sb[:, 2 * g : 2 * g + 2, :], in_=x_rows[:, 2 * g : 2 * g + 2, :])
+
+        def load_weight(w, words, scales):
+            nc.sync.dma_start(
+                out=w_bytes[:, w, :].bitcast(I32),
+                in_=words[0].rearrange("p n t -> p (n t)").bitcast(I32),
+            )
+            for quad in range(4):
+                nc.sync.dma_start(
+                    out=w_planes[32 * quad : 32 * quad + 4, w, :].bitcast(I32),
+                    in_=scales[0, 4 * quad : 4 * quad + 4, :].bitcast(I32),
+                )
+
+        load_x(0)
+        nc.sync.dma_start(out=b1_row[0:1, :], in_=b1.rearrange("(o f) -> o f", o=1))
+        load_weight(0, w1_words, w1_scales)
+        for g in range(1, PAIRS):
+            load_x(g)
+        load_weight(1, w2_words, w2_scales)
+        for v, vec in enumerate((b2, gamma, beta)):
+            nc.sync.dma_start(
+                out=vec_rows[FEAT_TILES * v : FEAT_TILES * (v + 1), :],
+                in_=vec.rearrange("(c m) -> c m", m=P),
+            )
+
+        b1_ps = psum.tile([P, FEAT], F32, tag="bank")
+        nc.tensor.matmul(out=b1_ps[:], lhsT=ones[:], rhs=b1_row[:], start=True, stop=True)
+        b1_sorted = keep.tile([P, 2, P, 2], F32)
+        nc.vector.tensor_copy(
+            out=b1_sorted[:], in_=b1_ps[:].rearrange("p (q u e) -> p u q e", u=2, e=2)
+        )
+
+        grouped_x, grouped_h, acc1, biased, h1 = {}, {}, {}, {}, {}
+
+        def flip(word_columns, grouped):
+            flipped = psum.tile([P, 2, 2, P], F32, tag="bank")
+            for a in range(2):
+                for u in range(2):
+                    nc.tensor.transpose(out=flipped[:, a, u, :], in_=word_columns(a, u), identity=ident[:])
+            nc.scalar.copy(out=grouped[:].bitcast(F32), in_=flipped[:].rearrange("p a u r -> p a r u"))
+
+        def quantise(g, grouped, codes, plane):
+            cols = slice(2 * P * g, 2 * P * (g + 1))
+            nc.vector.quantize_mx(
+                out=codes[:, cols].bitcast(FP8X4),
+                scales=plane[:, cols],
+                in_=grouped[:].rearrange("p a r t -> p (a r t)"),
+            )
+
+        def flip_x(g):
+            grouped_x[g] = work.tile([P, 2, P, PACK], BF16, name="grouped_x", align_bytes=64)
+            x_words = x_sb[:].bitcast(F32)
+            flip(lambda a, u: x_words[:, 2 * g + a, u:WORDS:2], grouped_x[g])
+
+        def multiply1(g):
+            for a in range(2):
+                i = 2 * g + a
+                acc1[i] = psum.tile([P, FEAT], F32, name="acc1", tag="bank")
+                nc.tensor.matmul_mx(
+                    out=acc1[i][:],
+                    lhsT=x_codes[:, P * i : P * (i + 1)].bitcast(FP8X4),
+                    lhsT_scale=x_plane[:, P * i : P * (i + 1)],
+                    rhs=w_bytes[:, 0, :].bitcast(FP8X4),
+                    rhs_scale=w_planes[:, 0, :],
+                    start=True,
+                    stop=True,
+                )
+
+        def add_bias1(g):
+            biased[g] = work.tile([P, 2, FEAT], F32, name="biased")
+            for a in range(2):
+                nc.vector.tensor_tensor(
+                    out=biased[g][:, a, :].rearrange("p (u q e) -> p u q e", u=2, e=2),
+                    in0=acc1[2 * g + a][:].rearrange("p (q u e) -> p u q e", u=2, e=2),
+                    in1=b1_sorted[:],
+                    op=ALU.add,
+                )
+
+        def leaky1(g):
+            h1[g] = work.tile([P, 2, FEAT], BF16, name="h1")
+            flat = biased[g][:].rearrange("p a f -> p (a f)")
+            nc.vector.scalar_tensor_tensor(
+                out=h1[g][:].rearrange("p a f -> p (a f)"),
+                in0=flat, scalar=SLOPE, in1=flat, op0=ALU.mult, op1=ALU.max,
+            )
+
+        def flip_h(g):
+            grouped_h[g] = work.tile([P, 2, P, PACK], BF16, name="grouped_h", align_bytes=64)
+            h1_words = h1[g][:].bitcast(F32)
+            flip(lambda a, u: h1_words[:, a, P * u : P * (u + 1)], grouped_h[g])
+
+        vec_cols = keep.tile([P, 3, FEAT_TILES], F32)
+        biased2 = {}
+
+        def spread_vectors():
+            vec_ps = psum.tile([P, P], BF16, tag="bank")
+            nc.tensor.transpose(out=vec_ps[:], in_=vec_rows[:], identity=ident_bf[:])
+            nc.vector.tensor_copy(
+                out=vec_cols[:].rearrange("p v c -> p (v c)"), in_=vec_ps[:, 0 : 3 * FEAT_TILES]
+            )
+
+        def multiply2(half, c):
+            rows = slice(HALF * half, HALF * (half + 1))
+            acc2 = psum.tile([P, HALF], F32, tag="bank")
+            nc.tensor.matmul_mx(
+                out=acc2[:],
+                lhsT=w_bytes[:, 1, PACK * P * c : PACK * P * (c + 1)].bitcast(FP8X4),
+                lhsT_scale=w_planes[:, 1, P * c : P * (c + 1)],
+                rhs=h_codes[:, rows].bitcast(FP8X4),
+                rhs_scale=h_plane[:, rows],
+                start=True,
+                stop=True,
+            )
+            biased2[half, c] = work.tile([P, HALF], F32, name="biased2", bufs=8)
+            nc.scalar.activation(
+                out=biased2[half, c][:], in_=acc2[:], func=ACT.Identity, bias=vec_cols[:, 0, c : c + 1]
+            )
+
+        def leaky2(half, c):
+            nc.vector.scalar_tensor_tensor(
+                out=h2[:, c, HALF * half : HALF * (half + 1)],
+                in0=biased2[half, c][:], scalar=SLOPE, in1=biased2[half, c][:],
+                op0=ALU.mult, op1=ALU.max,
+                accum_out=sums[:, c, half : half + 1],
+            )
+
+        normed, back = {}, {}
+
+        def stat(c, s):
+            return stats[:, c, s : s + 1]
+
+        NEG_MEAN, SQ_SUM, VAR_EPS, STD, RSTD, GAIN, SHIFT = range(7)
+
+        def mean(c):
+            nc.vector.tensor_scalar(
+                out=stat(c, NEG_MEAN), in0=sums[:, c, 0:1], scalar1=sums[:, c, 1:2], scalar2=-1.0 / ROWS,
+                op0=ALU.add, op1=ALU.mult,
+            )
+
+        def squares(c):
+            unread = work.tile([P, ROWS], BF16, name="unread")
+            nc.scalar.activation(
+                out=unread[:], in_=h2[:, c, :], func=ACT.Square, bias=stat(c, NEG_MEAN),
+                accum_out=stat(c, SQ_SUM),
+            )
+
+        def gain_and_shift(c):
+            nc.vector.tensor_scalar(
+                out=stat(c, VAR_EPS), in0=stat(c, SQ_SUM), scalar1=1.0 / ROWS, scalar2=EPS,
+                op0=ALU.mult, op1=ALU.add,
+            )
+            nc.scalar.activation(out=stat(c, STD), in_=stat(c, VAR_EPS), func=ACT.Sqrt)
+            nc.vector.reciprocal(out=stat(c, RSTD), in_=stat(c, STD))
+            nc.vector.tensor_tensor(
+                out=stat(c, GAIN), in0=stat(c, RSTD), in1=vec_cols[:, 1, c : c + 1], op=ALU.mult
+            )
+            nc.vector.scalar_tensor_tensor(
+                out=stat(c, SHIFT), in0=stat(c, NEG_MEAN), scalar=stat(c, GAIN),
+                in1=vec_cols[:, 2, c : c + 1], op0=ALU.mult, op1=ALU.add,
+            )
+
+        def normalise(c):
+            normed[c] = work.tile([P, ROWS], F32, name="normed")
+            nc.vector.tensor_scalar(
+                out=normed[c][:], in0=h2[:, c, :], scalar1=stat(c, GAIN), scalar2=stat(c, SHIFT),
+                op0=ALU.mult, op1=ALU.add,
+            )
+
+        def flip_back(c):
+            for b in range(2):
+                back[c, b] = psum.tile([P, 4, P], F32, name="back", tag="bank")
+                for j in range(4):
+                    i = 4 * b + j
+                    nc.tensor.transpose(
+                        out=back[c, b][:, j, :], in_=normed[c][:, P * i : P * (i + 1)], identity=ident[:]
+                    )
+
+        def store(c):
+            feats = slice(P * c, P * (c + 1))
+            nc.scalar.copy(out=out_sb[:, 0:4, feats], in_=back[c, 0][:])
+            nc.vector.tensor_copy(out=out_sb[:, 4:8, feats], in_=back[c, 1][:])
+            nc.sync.dma_start(out=out_rows[:, :, feats], in_=out_sb[:, :, feats])
+
+        for g in range(2):
+            flip_x(g)
+            quantise(g, grouped_x[g], x_codes, x_plane)
+        multiply1(0)
+        for g in range(PAIRS):
+            add_bias1(g)
+            if g >= 1:
+                quantise(g - 1, grouped_h[g - 1], h_codes, h_plane)
+            if g == PAIRS // 2:
+                spread_vectors()
+                for c in range(FEAT_TILES):
+                    multiply2(0, c)
+            leaky1(g)
+            if g + 2 < PAIRS:
+                flip_x(g + 2)
+                quantise(g + 2, grouped_x[g + 2], x_codes, x_plane)
+            if g + 1 < PAIRS:
+                multiply1(g + 1)
+            flip_h(g)
+        for c in range(FEAT_TILES):
+            leaky2(0, c)
+        quantise(PAIRS - 1, grouped_h[PAIRS - 1], h_codes, h_plane)
+        for c in range(FEAT_TILES):
+            multiply2(1, c)
+
+        leaky2(1, 0)
+        mean(0)
+        squares(0)
+        for c in range(FEAT_TILES):
+            if c + 1 < FEAT_TILES:
+                leaky2(1, c + 1)
+                mean(c + 1)
+            gain_and_shift(c)
+            if c + 1 < FEAT_TILES:
+                squares(c + 1)
+            normalise(c)
+            flip_back(c)
+            if c >= 1:
+                store(c - 1)
+        store(FEAT_TILES - 1)

@@ -53,12 +53,16 @@ def tile_attention_prop_pa_kernel(
         h2 = keep.tile([P, FEAT_TILES, ROWS], F32)
         sums = keep.tile([P, FEAT_TILES, HALVES], F32)
         stats = keep.tile([P, FEAT_TILES, 8], F32)
+        zero = keep.tile([P, 1], F32)
+        eps = keep.tile([P, 1], F32)
         out_sb = keep.tile([P, ROW_TILES, FEAT], F32)
 
         nc.vector.memset(w_planes[:].rearrange("p w n -> p (w n)").bitcast(I32), 0)
         nc.vector.memset(b1_row[:], 0.0)
         nc.vector.memset(ones[:], 1.0)
         nc.vector.memset(vec_rows[:], 0.0)
+        nc.vector.memset(zero[:], 0.0)
+        nc.vector.tensor_scalar(out=eps[:], in0=zero[:], scalar1=EPS, scalar2=None, op0=ALU.add)
         make_identity(nc, ident[:])
         nc.vector.tensor_copy(out=ident_bf[:], in_=ident[:])
         warm = keep.tile([P, 1], F32)
@@ -160,20 +164,20 @@ def tile_attention_prop_pa_kernel(
             flip(lambda a, u: h1_words[:, a, P * u : P * (u + 1)], grouped_h[g])
 
         vec_cols = keep.tile([P, 3, FEAT_TILES], F32)
-        biased2 = {}
+        acc2, biased2 = {}, {}
 
         def spread_vectors():
             vec_ps = psum.tile([P, P], BF16, tag="bank")
             nc.tensor.transpose(out=vec_ps[:], in_=vec_rows[:], identity=ident_bf[:])
-            nc.vector.tensor_copy(
+            nc.scalar.copy(
                 out=vec_cols[:].rearrange("p v c -> p (v c)"), in_=vec_ps[:, 0 : 3 * FEAT_TILES]
             )
 
         def multiply2(half, c):
             rows = slice(HALF * half, HALF * (half + 1))
-            acc2 = psum.tile([P, HALF], F32, tag="bank")
+            acc2[half, c] = psum.tile([P, HALF], F32, name="acc2", tag="bank")
             nc.tensor.matmul_mx(
-                out=acc2[:],
+                out=acc2[half, c][:],
                 lhsT=w_bytes[:, 1, PACK * P * c : PACK * P * (c + 1)].bitcast(FP8X4),
                 lhsT_scale=w_planes[:, 1, P * c : P * (c + 1)],
                 rhs=h_codes[:, rows].bitcast(FP8X4),
@@ -181,9 +185,12 @@ def tile_attention_prop_pa_kernel(
                 start=True,
                 stop=True,
             )
+
+        def add_bias2(half, c):
             biased2[half, c] = work.tile([P, HALF], F32, name="biased2", bufs=8)
             nc.scalar.activation(
-                out=biased2[half, c][:], in_=acc2[:], func=ACT.Identity, bias=vec_cols[:, 0, c : c + 1]
+                out=biased2[half, c][:], in_=acc2[half, c][:], func=ACT.Identity,
+                bias=vec_cols[:, 0, c : c + 1],
             )
 
         def leaky2(half, c):
@@ -199,7 +206,7 @@ def tile_attention_prop_pa_kernel(
         def stat(c, s):
             return stats[:, c, s : s + 1]
 
-        NEG_MEAN, SQ_SUM, VAR_EPS, STD, RSTD, GAIN, SHIFT = range(7)
+        NEG_MEAN, SQ_SUM, STD, RSTD, GAIN, SHIFT = range(6)
 
         def mean(c):
             nc.vector.tensor_scalar(
@@ -213,13 +220,11 @@ def tile_attention_prop_pa_kernel(
                 out=unread[:], in_=h2[:, c, :], func=ACT.Square, bias=stat(c, NEG_MEAN),
                 accum_out=stat(c, SQ_SUM),
             )
+            nc.scalar.activation(
+                out=stat(c, STD), in_=stat(c, SQ_SUM), func=ACT.Sqrt, scale=1.0 / ROWS, bias=eps[:]
+            )
 
         def gain_and_shift(c):
-            nc.vector.tensor_scalar(
-                out=stat(c, VAR_EPS), in0=stat(c, SQ_SUM), scalar1=1.0 / ROWS, scalar2=EPS,
-                op0=ALU.mult, op1=ALU.add,
-            )
-            nc.scalar.activation(out=stat(c, STD), in_=stat(c, VAR_EPS), func=ACT.Sqrt)
             nc.vector.reciprocal(out=stat(c, RSTD), in_=stat(c, STD))
             nc.vector.tensor_tensor(
                 out=stat(c, GAIN), in0=stat(c, RSTD), in1=vec_cols[:, 1, c : c + 1], op=ALU.mult
@@ -248,8 +253,9 @@ def tile_attention_prop_pa_kernel(
         def store(c):
             feats = slice(P * c, P * (c + 1))
             nc.scalar.copy(out=out_sb[:, 0:4, feats], in_=back[c, 0][:])
+            nc.sync.dma_start(out=out_rows[:, 0:4, feats], in_=out_sb[:, 0:4, feats])
             nc.vector.tensor_copy(out=out_sb[:, 4:8, feats], in_=back[c, 1][:])
-            nc.sync.dma_start(out=out_rows[:, :, feats], in_=out_sb[:, :, feats])
+            nc.sync.dma_start(out=out_rows[:, 4:8, feats], in_=out_sb[:, 4:8, feats])
 
         for g in range(2):
             flip_x(g)
@@ -263,6 +269,7 @@ def tile_attention_prop_pa_kernel(
                 spread_vectors()
                 for c in range(FEAT_TILES):
                     multiply2(0, c)
+                    add_bias2(0, c)
             leaky1(g)
             if g + 2 < PAIRS:
                 flip_x(g + 2)
@@ -276,10 +283,14 @@ def tile_attention_prop_pa_kernel(
         for c in range(FEAT_TILES):
             multiply2(1, c)
 
+        add_bias2(1, 0)
+        add_bias2(1, 1)
         leaky2(1, 0)
         mean(0)
         squares(0)
         for c in range(FEAT_TILES):
+            if c + 2 < FEAT_TILES:
+                add_bias2(1, c + 2)
             if c + 1 < FEAT_TILES:
                 leaky2(1, c + 1)
                 mean(c + 1)

@@ -263,42 +263,47 @@ def tile_attention_prop_pa_kernel(
         multiply1(0)
         for g in range(PAIRS):
             add_bias1(g)
+            leaky1(g)
             if g >= 1:
                 quantise(g - 1, grouped_h[g - 1], h_codes, h_plane)
-            if g == PAIRS // 2:
-                spread_vectors()
-                for c in range(FEAT_TILES):
-                    multiply2(0, c)
-                    add_bias2(0, c)
-            leaky1(g)
             if g + 2 < PAIRS:
                 flip_x(g + 2)
                 quantise(g + 2, grouped_x[g + 2], x_codes, x_plane)
             if g + 1 < PAIRS:
                 multiply1(g + 1)
             flip_h(g)
-        for c in range(FEAT_TILES):
+            if g == PAIRS // 2:
+                spread_vectors()
+                for c in range(FEAT_TILES):
+                    multiply2(0, c)
+                    add_bias2(0, c)
+        for c in range(FEAT_TILES // 2):
             leaky2(0, c)
         quantise(PAIRS - 1, grouped_h[PAIRS - 1], h_codes, h_plane)
         for c in range(FEAT_TILES):
             multiply2(1, c)
+        for c in range(FEAT_TILES // 2, FEAT_TILES):
+            leaky2(0, c)
 
-        add_bias2(1, 0)
-        add_bias2(1, 1)
-        leaky2(1, 0)
-        mean(0)
-        squares(0)
-        for c in range(FEAT_TILES):
-            if c + 2 < FEAT_TILES:
-                add_bias2(1, c + 2)
-            if c + 1 < FEAT_TILES:
-                leaky2(1, c + 1)
-                mean(c + 1)
-            gain_and_shift(c)
-            if c + 1 < FEAT_TILES:
-                squares(c + 1)
-            normalise(c)
-            flip_back(c)
-            if c >= 1:
-                store(c - 1)
-        store(FEAT_TILES - 1)
+        BIAS_AHEAD = 2
+        NORM_LAG = 2
+        STORE_LAG = 4
+
+        def tiles_at(c):
+            return [c] if 0 <= c < FEAT_TILES else []
+
+        for c in range(BIAS_AHEAD):
+            add_bias2(1, c)
+        for step in range(FEAT_TILES + STORE_LAG):
+            for c in tiles_at(step + BIAS_AHEAD):
+                add_bias2(1, c)
+            for c in tiles_at(step):
+                leaky2(1, c)
+                mean(c)
+                squares(c)
+            for c in tiles_at(step - NORM_LAG):
+                gain_and_shift(c)
+                normalise(c)
+                flip_back(c)
+            for c in tiles_at(step - STORE_LAG):
+                store(c)

@@ -41,8 +41,10 @@ def tile_attention_prop_pa_kernel(
         x_sb = keep.tile([P, ROW_TILES, FEAT], BF16)
         w_bytes = keep.tile([P, 2, PACK * FEAT], U8, align_bytes=64)
         w_planes = keep.tile([P, 2, FEAT], U8, align_bytes=64)
-        ones = keep.tile([P, P], BF16)
-        b1_row = keep.tile([P, FEAT], BF16)
+        w1_codes = keep.tile([P, FEAT], I32, align_bytes=64)
+        w1_plane = keep.tile([P, FEAT], U8, align_bytes=64)
+        b1_bf = keep.tile([P, PACK], BF16)
+        b1_cols = keep.tile([P, PACK], F32)
         vec_rows = keep.tile([P, P], BF16)
         ident = keep.tile([P, P], F32)
         ident_bf = keep.tile([P, P], BF16)
@@ -58,15 +60,15 @@ def tile_attention_prop_pa_kernel(
         out_sb = keep.tile([P, ROW_TILES, FEAT], F32)
 
         nc.vector.memset(w_planes[:].rearrange("p w n -> p (w n)").bitcast(I32), 0)
-        nc.vector.memset(b1_row[:], 0.0)
-        nc.vector.memset(ones[:], 1.0)
+        one = keep.tile([P, 1], F32)
+        nc.vector.memset(one[:], 1.0)
         nc.vector.memset(vec_rows[:], 0.0)
         nc.vector.memset(zero[:], 0.0)
         nc.vector.tensor_scalar(out=eps[:], in0=zero[:], scalar1=EPS, scalar2=None, op0=ALU.add)
         make_identity(nc, ident[:])
         nc.vector.tensor_copy(out=ident_bf[:], in_=ident[:])
         warm = keep.tile([P, 1], F32)
-        nc.scalar.activation(out=warm[:], in_=ones[:, 0:1], func=ACT.Sqrt)
+        nc.scalar.activation(out=warm[:], in_=one[:], func=ACT.Sqrt)
 
         x_rows = x.rearrange("(p i) k -> p i k", i=ROW_TILES)
         out_rows = out.rearrange("(p i) f -> p i f", i=ROW_TILES)
@@ -86,7 +88,7 @@ def tile_attention_prop_pa_kernel(
                 )
 
         load_x(0)
-        nc.sync.dma_start(out=b1_row[0:1, :], in_=b1.rearrange("(o f) -> o f", o=1))
+        nc.sync.dma_start(out=b1_bf[:], in_=b1.rearrange("(p t) -> p t", t=PACK))
         load_weight(0, w1_words, w1_scales)
         for g in range(1, PAIRS):
             load_x(g)
@@ -97,14 +99,18 @@ def tile_attention_prop_pa_kernel(
                 in_=vec.rearrange("(c m) -> c m", m=P),
             )
 
-        b1_ps = psum.tile([P, FEAT], F32, tag="bank")
-        nc.tensor.matmul(out=b1_ps[:], lhsT=ones[:], rhs=b1_row[:], start=True, stop=True)
-        b1_sorted = keep.tile([P, 2, P, 2], F32)
-        nc.vector.tensor_copy(
-            out=b1_sorted[:], in_=b1_ps[:].rearrange("p (q u e) -> p u q e", u=2, e=2)
-        )
+        def permute_w1():
+            nc.vector.tensor_copy(
+                out=w1_codes[:].rearrange("p (t m) -> p t m", t=PACK),
+                in_=w_bytes[:, 0, :].bitcast(I32).rearrange("p (m t) -> p t m", t=PACK),
+            )
+            nc.vector.tensor_copy(
+                out=w1_plane[:].rearrange("p (t m) -> p m t", t=PACK),
+                in_=w_planes[:, 0, :].rearrange("p (m t) -> p m t", t=PACK),
+            )
+            nc.vector.tensor_copy(out=b1_cols[:], in_=b1_bf[:])
 
-        grouped_x, grouped_h, acc1, biased, h1 = {}, {}, {}, {}, {}
+        grouped_x, grouped_h, acc1, biased = {}, {}, {}, {}
 
         def flip(word_columns, grouped):
             flipped = psum.tile([P, 2, 2, P], F32, tag="bank")
@@ -127,41 +133,43 @@ def tile_attention_prop_pa_kernel(
             flip(lambda a, u: x_words[:, 2 * g + a, u:WORDS:2], grouped_x[g])
 
         def multiply1(g):
-            for a in range(2):
-                i = 2 * g + a
-                acc1[i] = psum.tile([P, FEAT], F32, name="acc1", tag="bank")
-                nc.tensor.matmul_mx(
-                    out=acc1[i][:],
-                    lhsT=x_codes[:, P * i : P * (i + 1)].bitcast(FP8X4),
-                    lhsT_scale=x_plane[:, P * i : P * (i + 1)],
-                    rhs=w_bytes[:, 0, :].bitcast(FP8X4),
-                    rhs_scale=w_planes[:, 0, :],
-                    start=True,
-                    stop=True,
-                )
+            cols = slice(2 * P * g, 2 * P * (g + 1))
+            for b in range(2):
+                acc1[g, b] = psum.tile([P, 2, 2 * P], F32, name="acc1", tag="bank")
+                for s in range(2):
+                    t = 2 * b + s
+                    nc.tensor.matmul_mx(
+                        out=acc1[g, b][:, s, :],
+                        lhsT=w1_codes[:, P * t : P * (t + 1)].bitcast(FP8X4),
+                        lhsT_scale=w1_plane[:, P * t : P * (t + 1)],
+                        rhs=x_codes[:, cols].bitcast(FP8X4),
+                        rhs_scale=x_plane[:, cols],
+                        start=True,
+                        stop=True,
+                    )
 
         def add_bias1(g):
-            biased[g] = work.tile([P, 2, FEAT], F32, name="biased")
-            for a in range(2):
-                nc.vector.tensor_tensor(
-                    out=biased[g][:, a, :].rearrange("p (u q e) -> p u q e", u=2, e=2),
-                    in0=acc1[2 * g + a][:].rearrange("p (q u e) -> p u q e", u=2, e=2),
-                    in1=b1_sorted[:],
-                    op=ALU.add,
+            biased[g] = work.tile([P, PACK, 2 * P], F32, name="biased")
+            for t in range(PACK):
+                nc.scalar.activation(
+                    out=biased[g][:, t, :], in_=acc1[g, t // 2][:, t % 2, :], func=ACT.Identity,
+                    bias=b1_cols[:, t : t + 1],
                 )
 
         def leaky1(g):
-            h1[g] = work.tile([P, 2, FEAT], BF16, name="h1")
-            flat = biased[g][:].rearrange("p a f -> p (a f)")
+            grouped_h[g] = work.tile([P, 2 * P, PACK], BF16, name="grouped_h", align_bytes=64)
+            turned = biased[g][:].rearrange("p t r -> p r t")
             nc.vector.scalar_tensor_tensor(
-                out=h1[g][:].rearrange("p a f -> p (a f)"),
-                in0=flat, scalar=SLOPE, in1=flat, op0=ALU.mult, op1=ALU.max,
+                out=grouped_h[g][:], in0=turned, scalar=SLOPE, in1=turned, op0=ALU.mult, op1=ALU.max,
             )
 
-        def flip_h(g):
-            grouped_h[g] = work.tile([P, 2, P, PACK], BF16, name="grouped_h", align_bytes=64)
-            h1_words = h1[g][:].bitcast(F32)
-            flip(lambda a, u: h1_words[:, a, P * u : P * (u + 1)], grouped_h[g])
+        def quantise_h(g):
+            cols = slice(2 * P * g, 2 * P * (g + 1))
+            nc.vector.quantize_mx(
+                out=h_codes[:, cols].bitcast(FP8X4),
+                scales=h_plane[:, cols],
+                in_=grouped_h[g][:].rearrange("p r t -> p (r t)"),
+            )
 
         vec_cols = keep.tile([P, 3, FEAT_TILES], F32)
         acc2, biased2 = {}, {}
@@ -257,32 +265,30 @@ def tile_attention_prop_pa_kernel(
             nc.vector.tensor_copy(out=out_sb[:, 4:8, feats], in_=back[c, 1][:])
             nc.sync.dma_start(out=out_rows[:, 4:8, feats], in_=out_sb[:, 4:8, feats])
 
+        permute_w1()
         for g in range(2):
             flip_x(g)
             quantise(g, grouped_x[g], x_codes, x_plane)
         multiply1(0)
         for g in range(PAIRS):
             add_bias1(g)
-            leaky1(g)
-            if g >= 1:
-                quantise(g - 1, grouped_h[g - 1], h_codes, h_plane)
             if g + 2 < PAIRS:
                 flip_x(g + 2)
-                quantise(g + 2, grouped_x[g + 2], x_codes, x_plane)
             if g + 1 < PAIRS:
                 multiply1(g + 1)
-            flip_h(g)
-            if g == PAIRS // 2:
+            leaky1(g)
+            if g + 2 < PAIRS:
+                quantise(g + 2, grouped_x[g + 2], x_codes, x_plane)
+            if g == PAIRS - 1:
                 spread_vectors()
                 for c in range(FEAT_TILES):
                     multiply2(0, c)
                     add_bias2(0, c)
-        for c in range(FEAT_TILES // 2):
-            leaky2(0, c)
-        quantise(PAIRS - 1, grouped_h[PAIRS - 1], h_codes, h_plane)
+                leaky2(0, 0)
+            quantise_h(g)
         for c in range(FEAT_TILES):
             multiply2(1, c)
-        for c in range(FEAT_TILES // 2, FEAT_TILES):
+        for c in range(1, FEAT_TILES):
             leaky2(0, c)
 
         BIAS_AHEAD = 2

@@ -77,19 +77,19 @@ def tile_attention_prop_pa_kernel(
             nc.sync.dma_start(out=x_sb[:, 2 * g : 2 * g + 2, :], in_=x_rows[:, 2 * g : 2 * g + 2, :])
 
         def load_weight(w, words, scales):
-            nc.sync.dma_start(
-                out=w_bytes[:, w, :].bitcast(I32),
-                in_=words[0].rearrange("p n t -> p (n t)").bitcast(I32),
-            )
             for quad in range(4):
                 nc.sync.dma_start(
                     out=w_planes[32 * quad : 32 * quad + 4, w, :].bitcast(I32),
                     in_=scales[0, 4 * quad : 4 * quad + 4, :].bitcast(I32),
                 )
+            nc.sync.dma_start(
+                out=w_bytes[:, w, :].bitcast(I32),
+                in_=words[0].rearrange("p n t -> p (n t)").bitcast(I32),
+            )
 
         load_x(0)
-        nc.sync.dma_start(out=b1_bf[:], in_=b1.rearrange("(p t) -> p t", t=PACK))
         load_weight(0, w1_words, w1_scales)
+        nc.sync.dma_start(out=b1_bf[:], in_=b1.rearrange("(p t) -> p t", t=PACK))
         for g in range(1, PAIRS):
             load_x(g)
         load_weight(1, w2_words, w2_scales)
@@ -101,12 +101,12 @@ def tile_attention_prop_pa_kernel(
 
         def permute_w1():
             nc.vector.tensor_copy(
-                out=w1_codes[:].rearrange("p (t m) -> p t m", t=PACK),
-                in_=w_bytes[:, 0, :].bitcast(I32).rearrange("p (m t) -> p t m", t=PACK),
+                out=w1_plane[:].rearrange("p (t m) -> p t m", t=PACK),
+                in_=w_planes[:, 0, :].rearrange("p (m t) -> p t m", t=PACK),
             )
             nc.vector.tensor_copy(
-                out=w1_plane[:].rearrange("p (t m) -> p m t", t=PACK),
-                in_=w_planes[:, 0, :].rearrange("p (m t) -> p m t", t=PACK),
+                out=w1_codes[:].rearrange("p (t m) -> p t m", t=PACK),
+                in_=w_bytes[:, 0, :].bitcast(I32).rearrange("p (m t) -> p t m", t=PACK),
             )
             nc.vector.tensor_copy(out=b1_cols[:], in_=b1_bf[:])
 

@@ -54,7 +54,12 @@ def tile_attention_prop_pa_kernel(
         h_plane = keep.tile([P, ROWS], U8, align_bytes=64)
         h2 = keep.tile([P, FEAT_TILES, ROWS], F32)
         sums = keep.tile([P, FEAT_TILES, HALVES], F32)
+        square_sums = keep.tile([P, FEAT_TILES, HALVES], F32)
         stats = keep.tile([P, FEAT_TILES, 8], F32)
+        half_gamma = keep.tile([P, FEAT_TILES], F32)
+        factors = keep.tile([P, FEAT_TILES, 2], F32)
+        offsets = keep.tile([P, FEAT_TILES, 2], F32)
+        affine = keep.tile([P, FEAT_TILES, 2], F32)
         zero = keep.tile([P, 1], F32)
         eps = keep.tile([P, 1], F32)
         out_sb = keep.tile([P, ROW_TILES, FEAT], F32)
@@ -64,7 +69,7 @@ def tile_attention_prop_pa_kernel(
         nc.vector.memset(one[:], 1.0)
         nc.vector.memset(vec_rows[:], 0.0)
         nc.vector.memset(zero[:], 0.0)
-        nc.vector.tensor_scalar(out=eps[:], in0=zero[:], scalar1=EPS, scalar2=None, op0=ALU.add)
+        nc.vector.memset(offsets[:], 0.0)
         make_identity(nc, ident[:])
         nc.vector.tensor_copy(out=ident_bf[:], in_=ident[:])
         warm = keep.tile([P, 1], F32)
@@ -180,6 +185,15 @@ def tile_attention_prop_pa_kernel(
             nc.scalar.copy(
                 out=vec_cols[:].rearrange("p v c -> p (v c)"), in_=vec_ps[:, 0 : 3 * FEAT_TILES]
             )
+            nc.gpsimd.tensor_scalar(
+                out=half_gamma[:], in0=vec_cols[:, 1, :], scalar1=0.5, scalar2=0.0,
+                op0=ALU.mult, op1=ALU.add,
+            )
+            nc.gpsimd.tensor_scalar(
+                out=factors[:, :, 0], in0=vec_cols[:, 1, :], scalar1=float(HALF), scalar2=0.0,
+                op0=ALU.mult, op1=ALU.add,
+            )
+            nc.gpsimd.tensor_copy(out=offsets[:, :, 1], in_=vec_cols[:, 2, :])
 
         def multiply2(half, c):
             rows = slice(HALF * half, HALF * (half + 1))
@@ -214,56 +228,71 @@ def tile_attention_prop_pa_kernel(
         def stat(c, s):
             return stats[:, c, s : s + 1]
 
-        NEG_MEAN, SQ_SUM, STD, RSTD, GAIN, SHIFT = range(6)
+        FIRST, APART, KNOWN, STD, RSTD = range(5)
 
-        def mean(c):
-            nc.vector.tensor_scalar(
-                out=stat(c, NEG_MEAN), in0=sums[:, c, 0:1], scalar1=sums[:, c, 1:2], scalar2=-1.0 / ROWS,
-                op0=ALU.add, op1=ALU.mult,
+        def squares(half, c):
+            unread = work.tile([P, HALF], BF16, name="unread")
+            nc.scalar.activation(
+                out=unread[:], in_=h2[:, c, HALF * half : HALF * (half + 1)], func=ACT.Square,
+                scale=-float(HALF), bias=sums[:, c, half : half + 1],
+                accum_out=square_sums[:, c, half : half + 1],
             )
 
-        def squares(c):
-            unread = work.tile([P, ROWS], BF16, name="unread")
-            nc.scalar.activation(
-                out=unread[:], in_=h2[:, c, :], func=ACT.Square, bias=stat(c, NEG_MEAN),
-                accum_out=stat(c, SQ_SUM),
+        def first_half(c):
+            nc.gpsimd.tensor_scalar(
+                out=stat(c, FIRST), in0=square_sums[:, c, 0:1], scalar1=1.0 / ROWS,
+                scalar2=EPS * HALF * HALF, op0=ALU.mult, op1=ALU.add,
             )
+
+        def both_sums(c):
+            nc.gpsimd.tensor_scalar(
+                out=stat(c, APART), in0=sums[:, c, 1:2], scalar1=sums[:, c, 0:1], scalar2=0.5,
+                op0=ALU.subtract, op1=ALU.mult,
+            )
+            nc.gpsimd.tensor_scalar(
+                out=stat(c, KNOWN), in0=stat(c, APART), scalar1=stat(c, APART), scalar2=stat(c, FIRST),
+                op0=ALU.mult, op1=ALU.add,
+            )
+            nc.gpsimd.tensor_scalar(
+                out=factors[:, c, 1:2], in0=sums[:, c, 1:2], scalar1=sums[:, c, 0:1],
+                scalar2=half_gamma[:, c : c + 1], op0=ALU.add, op1=ALU.mult,
+            )
+
+        def deviation(c):
             nc.scalar.activation(
-                out=stat(c, STD), in_=stat(c, SQ_SUM), func=ACT.Sqrt, scale=1.0 / ROWS, bias=eps[:]
+                out=stat(c, STD), in_=square_sums[:, c, 1:2], func=ACT.Sqrt, scale=1.0 / ROWS,
+                bias=stat(c, KNOWN),
             )
 
         def gain_and_shift(c):
             nc.vector.reciprocal(out=stat(c, RSTD), in_=stat(c, STD))
-            nc.vector.tensor_tensor(
-                out=stat(c, GAIN), in0=stat(c, RSTD), in1=vec_cols[:, 1, c : c + 1], op=ALU.mult
-            )
             nc.vector.scalar_tensor_tensor(
-                out=stat(c, SHIFT), in0=stat(c, NEG_MEAN), scalar=stat(c, GAIN),
-                in1=vec_cols[:, 2, c : c + 1], op0=ALU.mult, op1=ALU.add,
+                out=affine[:, c, :], in0=factors[:, c, :], scalar=stat(c, RSTD), in1=offsets[:, c, :],
+                op0=ALU.mult, op1=ALU.subtract,
             )
 
-        def normalise(c):
-            normed[c] = work.tile([P, ROWS], F32, name="normed")
+        def normalise(c, b):
+            if b == 0:
+                normed[c] = work.tile([P, ROWS], F32, name="normed")
+            rows = slice(HALF * b, HALF * (b + 1))
             nc.vector.tensor_scalar(
-                out=normed[c][:], in0=h2[:, c, :], scalar1=stat(c, GAIN), scalar2=stat(c, SHIFT),
-                op0=ALU.mult, op1=ALU.add,
+                out=normed[c][:, rows], in0=h2[:, c, rows], scalar1=affine[:, c, 0:1],
+                scalar2=affine[:, c, 1:2], op0=ALU.mult, op1=ALU.subtract,
             )
 
-        def flip_back(c):
-            for b in range(2):
-                back[c, b] = psum.tile([P, 4, P], F32, name="back", tag="bank")
-                for j in range(4):
-                    i = 4 * b + j
-                    nc.tensor.transpose(
-                        out=back[c, b][:, j, :], in_=normed[c][:, P * i : P * (i + 1)], identity=ident[:]
-                    )
+        def flip_back(c, b):
+            back[c, b] = psum.tile([P, 4, P], F32, name="back", tag="bank")
+            for j in range(4):
+                i = 4 * b + j
+                nc.tensor.transpose(
+                    out=back[c, b][:, j, :], in_=normed[c][:, P * i : P * (i + 1)], identity=ident[:]
+                )
 
-        def store(c):
+        def store(c, b, copier):
             feats = slice(P * c, P * (c + 1))
-            nc.scalar.copy(out=out_sb[:, 0:4, feats], in_=back[c, 0][:])
-            nc.sync.dma_start(out=out_rows[:, 0:4, feats], in_=out_sb[:, 0:4, feats])
-            nc.vector.tensor_copy(out=out_sb[:, 4:8, feats], in_=back[c, 1][:])
-            nc.sync.dma_start(out=out_rows[:, 4:8, feats], in_=out_sb[:, 4:8, feats])
+            tiles = slice(4 * b, 4 * (b + 1))
+            copier(out=out_sb[:, tiles, feats], in_=back[c, b][:])
+            nc.sync.dma_start(out=out_rows[:, tiles, feats], in_=out_sb[:, tiles, feats])
 
         permute_w1()
         for g in range(2):
@@ -288,28 +317,53 @@ def tile_attention_prop_pa_kernel(
             quantise_h(g)
         for c in range(FEAT_TILES):
             multiply2(1, c)
-        for c in range(1, FEAT_TILES):
-            leaky2(0, c)
 
-        BIAS_AHEAD = 2
-        NORM_LAG = 2
-        STORE_LAG = 4
+        def norm(c):
+            gain_and_shift(c)
+            for b in range(2):
+                normalise(c, b)
+                flip_back(c, b)
 
-        def tiles_at(c):
-            return [c] if 0 <= c < FEAT_TILES else []
-
-        for c in range(BIAS_AHEAD):
-            add_bias2(1, c)
-        for step in range(FEAT_TILES + STORE_LAG):
-            for c in tiles_at(step + BIAS_AHEAD):
-                add_bias2(1, c)
-            for c in tiles_at(step):
-                leaky2(1, c)
-                mean(c)
-                squares(c)
-            for c in tiles_at(step - NORM_LAG):
-                gain_and_shift(c)
-                normalise(c)
-                flip_back(c)
-            for c in tiles_at(step - STORE_LAG):
-                store(c)
+        squares(0, 0)
+        first_half(0)
+        add_bias2(1, 0)
+        leaky2(0, 1)
+        leaky2(0, 2)
+        squares(0, 1)
+        first_half(1)
+        leaky2(1, 0)
+        both_sums(0)
+        add_bias2(1, 1)
+        squares(1, 0)
+        deviation(0)
+        leaky2(0, 3)
+        squares(0, 2)
+        first_half(2)
+        leaky2(1, 1)
+        both_sums(1)
+        add_bias2(1, 2)
+        norm(0)
+        squares(1, 1)
+        deviation(1)
+        squares(0, 3)
+        first_half(3)
+        leaky2(1, 2)
+        both_sums(2)
+        add_bias2(1, 3)
+        store(0, 0, nc.scalar.copy)
+        norm(1)
+        squares(1, 2)
+        deviation(2)
+        leaky2(1, 3)
+        both_sums(3)
+        store(0, 1, nc.vector.tensor_copy)
+        squares(1, 3)
+        deviation(3)
+        norm(2)
+        store(1, 0, nc.scalar.copy)
+        store(1, 1, nc.vector.tensor_copy)
+        norm(3)
+        store(2, 0, nc.scalar.copy)
+        store(2, 1, nc.vector.tensor_copy)
+        store(3, 0, nc.scalar.copy)
+        store(3, 1, nc.vector.tensor_copy)

@@ -53,13 +53,13 @@ def tile_attention_prop_pa_kernel(
         h_codes = keep.tile([P, ROWS], U32, align_bytes=64)
         h_plane = keep.tile([P, ROWS], U8, align_bytes=64)
         h2 = keep.tile([P, FEAT_TILES, ROWS], F32)
-        sums = keep.tile([P, FEAT_TILES, HALVES], F32)
-        square_sums = keep.tile([P, FEAT_TILES, HALVES], F32)
+        triples = keep.tile([P, FEAT_TILES, HALVES, 3], F32)
+        mean_var = keep.tile([P, FEAT_TILES, 2], F32)
         stats = keep.tile([P, FEAT_TILES, 8], F32)
-        half_gamma = keep.tile([P, FEAT_TILES], F32)
-        factors = keep.tile([P, FEAT_TILES, 2], F32)
-        offsets = keep.tile([P, FEAT_TILES, 2], F32)
-        affine = keep.tile([P, FEAT_TILES, 2], F32)
+        factors = keep.tile([P, 2, FEAT_TILES], F32)
+        affine = keep.tile([P, 2, FEAT_TILES], F32)
+        std = keep.tile([P, FEAT_TILES], F32)
+        rstd = keep.tile([P, FEAT_TILES], F32)
         zero = keep.tile([P, 1], F32)
         eps = keep.tile([P, 1], F32)
         out_sb = keep.tile([P, ROW_TILES, FEAT], F32)
@@ -69,7 +69,10 @@ def tile_attention_prop_pa_kernel(
         nc.vector.memset(one[:], 1.0)
         nc.vector.memset(vec_rows[:], 0.0)
         nc.vector.memset(zero[:], 0.0)
-        nc.vector.memset(offsets[:], 0.0)
+        nc.vector.memset(triples[:], float(HALF))
+        nc.vector.tensor_scalar(
+            out=eps[:], in0=zero[:], scalar1=EPS * HALF * HALF, scalar2=None, op0=ALU.add
+        )
         make_identity(nc, ident[:])
         nc.vector.tensor_copy(out=ident_bf[:], in_=ident[:])
         warm = keep.tile([P, 1], F32)
@@ -185,15 +188,9 @@ def tile_attention_prop_pa_kernel(
             nc.scalar.copy(
                 out=vec_cols[:].rearrange("p v c -> p (v c)"), in_=vec_ps[:, 0 : 3 * FEAT_TILES]
             )
-            nc.gpsimd.tensor_scalar(
-                out=half_gamma[:], in0=vec_cols[:, 1, :], scalar1=0.5, scalar2=0.0,
-                op0=ALU.mult, op1=ALU.add,
+            nc.scalar.activation(
+                out=factors[:, 0, :], in_=vec_cols[:, 1, :], func=ACT.Copy, scale=float(HALF)
             )
-            nc.gpsimd.tensor_scalar(
-                out=factors[:, :, 0], in0=vec_cols[:, 1, :], scalar1=float(HALF), scalar2=0.0,
-                op0=ALU.mult, op1=ALU.add,
-            )
-            nc.gpsimd.tensor_copy(out=offsets[:, :, 1], in_=vec_cols[:, 2, :])
 
         def multiply2(half, c):
             rows = slice(HALF * half, HALF * (half + 1))
@@ -208,19 +205,25 @@ def tile_attention_prop_pa_kernel(
                 stop=True,
             )
 
-        def add_bias2(half, c):
+        def add_bias2(half, c, on_vector=False):
             biased2[half, c] = work.tile([P, HALF], F32, name="biased2", bufs=8)
-            nc.scalar.activation(
-                out=biased2[half, c][:], in_=acc2[half, c][:], func=ACT.Identity,
-                bias=vec_cols[:, 0, c : c + 1],
-            )
+            if on_vector:
+                nc.vector.tensor_scalar(
+                    out=biased2[half, c][:], in0=acc2[half, c][:], scalar1=vec_cols[:, 0, c : c + 1],
+                    scalar2=None, op0=ALU.add,
+                )
+            else:
+                nc.scalar.activation(
+                    out=biased2[half, c][:], in_=acc2[half, c][:], func=ACT.Identity,
+                    bias=vec_cols[:, 0, c : c + 1],
+                )
 
         def leaky2(half, c):
             nc.vector.scalar_tensor_tensor(
                 out=h2[:, c, HALF * half : HALF * (half + 1)],
                 in0=biased2[half, c][:], scalar=SLOPE, in1=biased2[half, c][:],
                 op0=ALU.mult, op1=ALU.max,
-                accum_out=sums[:, c, half : half + 1],
+                accum_out=triples[:, c, half, 1:2],
             )
 
         normed, back = {}, {}
@@ -228,71 +231,54 @@ def tile_attention_prop_pa_kernel(
         def stat(c, s):
             return stats[:, c, s : s + 1]
 
-        FIRST, APART, KNOWN, STD, RSTD = range(5)
+        STD, RSTD = range(2)
 
         def squares(half, c):
             unread = work.tile([P, HALF], BF16, name="unread")
             nc.scalar.activation(
                 out=unread[:], in_=h2[:, c, HALF * half : HALF * (half + 1)], func=ACT.Square,
-                scale=-float(HALF), bias=sums[:, c, half : half + 1],
-                accum_out=square_sums[:, c, half : half + 1],
+                scale=-float(HALF), bias=triples[:, c, half, 1:2],
+                accum_out=triples[:, c, half, 2:3],
             )
 
-        def first_half(c):
-            nc.gpsimd.tensor_scalar(
-                out=stat(c, FIRST), in0=square_sums[:, c, 0:1], scalar1=1.0 / ROWS,
-                scalar2=EPS * HALF * HALF, op0=ALU.mult, op1=ALU.add,
+        def aggregate(c):
+            nc.vector.bn_aggr(out=mean_var[:, c, :], in_=triples[:, c, :, :].rearrange("p h s -> p (h s)"))
+
+        def gain_and_shift():
+            nc.scalar.activation(out=std[:], in_=mean_var[:, :, 1], func=ACT.Sqrt, bias=eps[:])
+            nc.vector.tensor_tensor(
+                out=factors[:, 1, :], in0=mean_var[:, :, 0], in1=vec_cols[:, 1, :], op=ALU.mult
+            )
+            nc.vector.reciprocal(out=rstd[:], in_=std[:])
+            for s in range(2):
+                nc.vector.tensor_tensor(out=affine[:, s, :], in0=factors[:, s, :], in1=rstd[:], op=ALU.mult)
+            nc.vector.tensor_tensor(
+                out=affine[:, 1, :], in0=affine[:, 1, :], in1=vec_cols[:, 2, :], op=ALU.subtract
             )
 
-        def both_sums(c):
-            nc.gpsimd.tensor_scalar(
-                out=stat(c, APART), in0=sums[:, c, 1:2], scalar1=sums[:, c, 0:1], scalar2=0.5,
-                op0=ALU.subtract, op1=ALU.mult,
-            )
-            nc.gpsimd.tensor_scalar(
-                out=stat(c, KNOWN), in0=stat(c, APART), scalar1=stat(c, APART), scalar2=stat(c, FIRST),
-                op0=ALU.mult, op1=ALU.add,
-            )
-            nc.gpsimd.tensor_scalar(
-                out=factors[:, c, 1:2], in0=sums[:, c, 1:2], scalar1=sums[:, c, 0:1],
-                scalar2=half_gamma[:, c : c + 1], op0=ALU.add, op1=ALU.mult,
-            )
+        QUARTER = ROWS // 4
 
-        def deviation(c):
-            nc.scalar.activation(
-                out=stat(c, STD), in_=square_sums[:, c, 1:2], func=ACT.Sqrt, scale=1.0 / ROWS,
-                bias=stat(c, KNOWN),
-            )
-
-        def gain_and_shift(c):
-            nc.vector.reciprocal(out=stat(c, RSTD), in_=stat(c, STD))
-            nc.vector.scalar_tensor_tensor(
-                out=affine[:, c, :], in0=factors[:, c, :], scalar=stat(c, RSTD), in1=offsets[:, c, :],
-                op0=ALU.mult, op1=ALU.subtract,
-            )
-
-        def normalise(c, b):
-            if b == 0:
-                normed[c] = work.tile([P, ROWS], F32, name="normed")
-            rows = slice(HALF * b, HALF * (b + 1))
+        def normalise(c, q, on_scalar=False):
+            if c == 0:
+                normed[q] = work.tile([P, FEAT_TILES, QUARTER], F32, name="normed")
+            rows = slice(QUARTER * q, QUARTER * (q + 1))
             nc.vector.tensor_scalar(
-                out=normed[c][:, rows], in0=h2[:, c, rows], scalar1=affine[:, c, 0:1],
-                scalar2=affine[:, c, 1:2], op0=ALU.mult, op1=ALU.subtract,
+                out=normed[q][:, c, :], in0=h2[:, c, rows], scalar1=affine[:, 0, c : c + 1],
+                scalar2=affine[:, 1, c : c + 1], op0=ALU.mult, op1=ALU.subtract,
             )
 
-        def flip_back(c, b):
-            back[c, b] = psum.tile([P, 4, P], F32, name="back", tag="bank")
-            for j in range(4):
-                i = 4 * b + j
+        def flip_back(i):
+            back[i] = psum.tile([P, FEAT_TILES, P], F32, name="back", tag="bank")
+            for c in range(FEAT_TILES):
                 nc.tensor.transpose(
-                    out=back[c, b][:, j, :], in_=normed[c][:, P * i : P * (i + 1)], identity=ident[:]
+                    out=back[i][:, c, :], in_=normed[i // 2][:, c, P * (i % 2) : P * (i % 2 + 1)],
+                    identity=ident[:],
                 )
 
-        def store(c, b, copier):
-            feats = slice(P * c, P * (c + 1))
-            tiles = slice(4 * b, 4 * (b + 1))
-            copier(out=out_sb[:, tiles, feats], in_=back[c, b][:])
-            nc.sync.dma_start(out=out_rows[:, tiles, feats], in_=out_sb[:, tiles, feats])
+        def leave(i, copier):
+            copier(out=out_sb[:, i, :], in_=back[i][:].rearrange("p c m -> p (c m)"))
+            nc.sync.dma_start(out=out_rows[:, i, :], in_=out_sb[:, i, :])
+
 
         permute_w1()
         for g in range(2):
@@ -318,52 +304,39 @@ def tile_attention_prop_pa_kernel(
         for c in range(FEAT_TILES):
             multiply2(1, c)
 
-        def norm(c):
-            gain_and_shift(c)
-            for b in range(2):
-                normalise(c, b)
-                flip_back(c, b)
-
         squares(0, 0)
-        first_half(0)
         add_bias2(1, 0)
         leaky2(0, 1)
         leaky2(0, 2)
         squares(0, 1)
-        first_half(1)
+        add_bias2(1, 2, True)
         leaky2(1, 0)
-        both_sums(0)
         add_bias2(1, 1)
-        squares(1, 0)
-        deviation(0)
-        leaky2(0, 3)
         squares(0, 2)
-        first_half(2)
+        leaky2(0, 3)
+        squares(1, 0)
+        add_bias2(1, 3, True)
         leaky2(1, 1)
-        both_sums(1)
-        add_bias2(1, 2)
-        norm(0)
-        squares(1, 1)
-        deviation(1)
+        aggregate(0)
         squares(0, 3)
-        first_half(3)
+        squares(1, 1)
         leaky2(1, 2)
-        both_sums(2)
-        add_bias2(1, 3)
-        store(0, 0, nc.scalar.copy)
-        norm(1)
-        squares(1, 2)
-        deviation(2)
+        aggregate(1)
         leaky2(1, 3)
-        both_sums(3)
-        store(0, 1, nc.vector.tensor_copy)
+        squares(1, 2)
         squares(1, 3)
-        deviation(3)
-        norm(2)
-        store(1, 0, nc.scalar.copy)
-        store(1, 1, nc.vector.tensor_copy)
-        norm(3)
-        store(2, 0, nc.scalar.copy)
-        store(2, 1, nc.vector.tensor_copy)
-        store(3, 0, nc.scalar.copy)
-        store(3, 1, nc.vector.tensor_copy)
+        aggregate(2)
+        aggregate(3)
+        gain_and_shift()
+
+        on_scalar, on_vector = nc.scalar.copy, nc.vector.tensor_copy
+        for q in range(4):
+            for c in range(FEAT_TILES):
+                normalise(c, q)
+            flip_back(2 * q)
+            flip_back(2 * q + 1)
+            if q >= 1:
+                leave(2 * q - 2, on_scalar)
+                leave(2 * q - 1, on_scalar if q % 2 else on_vector)
+        leave(6, on_scalar)
+        leave(7, on_vector)

@@ -53,13 +53,14 @@ def tile_attention_prop_pa_kernel(
         h_codes = keep.tile([P, ROWS], U32, align_bytes=64)
         h_plane = keep.tile([P, ROWS], U8, align_bytes=64)
         h2 = keep.tile([P, FEAT_TILES, ROWS], F32)
-        triples = keep.tile([P, FEAT_TILES, HALVES, 3], F32)
-        mean_var = keep.tile([P, FEAT_TILES, 2], F32)
+        sums = keep.tile([P, FEAT_TILES, HALVES], F32)
+        square_sums = keep.tile([P, FEAT_TILES, HALVES], F32)
+        first_part = keep.tile([P, FEAT_TILES], F32)
+        neg_half_gamma = keep.tile([P, FEAT_TILES], F32)
+        offsets = keep.tile([P, FEAT_TILES, 2], F32)
         stats = keep.tile([P, FEAT_TILES, 8], F32)
-        factors = keep.tile([P, 2, FEAT_TILES], F32)
-        affine = keep.tile([P, 2, FEAT_TILES], F32)
-        std = keep.tile([P, FEAT_TILES], F32)
-        rstd = keep.tile([P, FEAT_TILES], F32)
+        factors = keep.tile([P, FEAT_TILES, 2], F32)
+        affine = keep.tile([P, FEAT_TILES, 2], F32)
         zero = keep.tile([P, 1], F32)
         eps = keep.tile([P, 1], F32)
         out_sb = keep.tile([P, ROW_TILES, FEAT], F32)
@@ -69,14 +70,11 @@ def tile_attention_prop_pa_kernel(
         nc.vector.memset(one[:], 1.0)
         nc.vector.memset(vec_rows[:], 0.0)
         nc.vector.memset(zero[:], 0.0)
-        nc.vector.memset(triples[:], float(HALF))
-        nc.vector.tensor_scalar(
-            out=eps[:], in0=zero[:], scalar1=EPS * HALF * HALF, scalar2=None, op0=ALU.add
-        )
+        nc.vector.memset(offsets[:], 0.0)
         make_identity(nc, ident[:])
         nc.vector.tensor_copy(out=ident_bf[:], in_=ident[:])
         warm = keep.tile([P, 1], F32)
-        nc.scalar.activation(out=warm[:], in_=one[:], func=ACT.Sqrt)
+        nc.scalar.activation(out=warm[:], in_=one[:], func=ACT.Abs_reciprocal_sqrt)
 
         x_rows = x.rearrange("(p i) k -> p i k", i=ROW_TILES)
         out_rows = out.rearrange("(p i) f -> p i f", i=ROW_TILES)
@@ -189,8 +187,10 @@ def tile_attention_prop_pa_kernel(
                 out=vec_cols[:].rearrange("p v c -> p (v c)"), in_=vec_ps[:, 0 : 3 * FEAT_TILES]
             )
             nc.scalar.activation(
-                out=factors[:, 0, :], in_=vec_cols[:, 1, :], func=ACT.Copy, scale=float(HALF)
+                out=factors[:, :, 0], in_=vec_cols[:, 1, :], func=ACT.Copy, scale=float(HALF)
             )
+            nc.scalar.activation(out=neg_half_gamma[:], in_=vec_cols[:, 1, :], func=ACT.Copy, scale=-0.5)
+            nc.scalar.copy(out=offsets[:, :, 1], in_=vec_cols[:, 2, :])
 
         def multiply2(half, c):
             rows = slice(HALF * half, HALF * (half + 1))
@@ -223,7 +223,7 @@ def tile_attention_prop_pa_kernel(
                 out=h2[:, c, HALF * half : HALF * (half + 1)],
                 in0=biased2[half, c][:], scalar=SLOPE, in1=biased2[half, c][:],
                 op0=ALU.mult, op1=ALU.max,
-                accum_out=triples[:, c, half, 1:2],
+                accum_out=sums[:, c, half : half + 1],
             )
 
         normed, back = {}, {}
@@ -231,29 +231,48 @@ def tile_attention_prop_pa_kernel(
         def stat(c, s):
             return stats[:, c, s : s + 1]
 
-        STD, RSTD = range(2)
+        HALF_GAP, KNOWN, RSTD = range(3)
 
         def squares(half, c):
             unread = work.tile([P, HALF], BF16, name="unread")
             nc.scalar.activation(
                 out=unread[:], in_=h2[:, c, HALF * half : HALF * (half + 1)], func=ACT.Square,
-                scale=-float(HALF), bias=triples[:, c, half, 1:2],
-                accum_out=triples[:, c, half, 2:3],
+                scale=-float(HALF), bias=sums[:, c, half : half + 1],
+                accum_out=square_sums[:, c, half : half + 1],
             )
 
-        def aggregate(c):
-            nc.vector.bn_aggr(out=mean_var[:, c, :], in_=triples[:, c, :, :].rearrange("p h s -> p (h s)"))
-
-        def gain_and_shift():
-            nc.scalar.activation(out=std[:], in_=mean_var[:, :, 1], func=ACT.Sqrt, bias=eps[:])
-            nc.vector.tensor_tensor(
-                out=factors[:, 1, :], in0=mean_var[:, :, 0], in1=vec_cols[:, 1, :], op=ALU.mult
+        def first_squares():
+            nc.vector.tensor_scalar(
+                out=first_part[:], in0=square_sums[:, :, 0], scalar1=1.0 / ROWS,
+                scalar2=EPS * HALF * HALF, op0=ALU.mult, op1=ALU.add,
             )
-            nc.vector.reciprocal(out=rstd[:], in_=std[:])
-            for s in range(2):
-                nc.vector.tensor_tensor(out=affine[:, s, :], in0=factors[:, s, :], in1=rstd[:], op=ALU.mult)
-            nc.vector.tensor_tensor(
-                out=affine[:, 1, :], in0=affine[:, 1, :], in1=vec_cols[:, 2, :], op=ALU.subtract
+
+        def both_sums(c):
+            nc.vector.tensor_scalar(
+                out=stat(c, HALF_GAP), in0=sums[:, c, 1:2], scalar1=sums[:, c, 0:1], scalar2=0.5,
+                op0=ALU.subtract, op1=ALU.mult,
+            )
+            nc.vector.tensor_scalar(
+                out=factors[:, c, 1:2], in0=sums[:, c, 1:2], scalar1=sums[:, c, 0:1],
+                scalar2=neg_half_gamma[:, c : c + 1], op0=ALU.add, op1=ALU.mult,
+            )
+
+        def known(c):
+            nc.vector.tensor_scalar(
+                out=stat(c, KNOWN), in0=stat(c, HALF_GAP), scalar1=stat(c, HALF_GAP),
+                scalar2=first_part[:, c : c + 1], op0=ALU.mult, op1=ALU.add,
+            )
+
+        def inverse_deviation(c):
+            nc.scalar.activation(
+                out=stat(c, RSTD), in_=square_sums[:, c, 1:2], func=ACT.Abs_reciprocal_sqrt,
+                scale=1.0 / ROWS, bias=stat(c, KNOWN),
+            )
+
+        def gain_and_shift(c):
+            nc.vector.scalar_tensor_tensor(
+                out=affine[:, c, :], in0=factors[:, c, :], scalar=stat(c, RSTD), in1=offsets[:, c, :],
+                op0=ALU.mult, op1=ALU.add,
             )
 
         QUARTER = ROWS // 4
@@ -263,8 +282,8 @@ def tile_attention_prop_pa_kernel(
                 normed[q] = work.tile([P, FEAT_TILES, QUARTER], F32, name="normed")
             rows = slice(QUARTER * q, QUARTER * (q + 1))
             nc.vector.tensor_scalar(
-                out=normed[q][:, c, :], in0=h2[:, c, rows], scalar1=affine[:, 0, c : c + 1],
-                scalar2=affine[:, 1, c : c + 1], op0=ALU.mult, op1=ALU.subtract,
+                out=normed[q][:, c, :], in0=h2[:, c, rows], scalar1=affine[:, c, 0:1],
+                scalar2=affine[:, c, 1:2], op0=ALU.mult, op1=ALU.add,
             )
 
         def flip_back(i):
@@ -314,20 +333,32 @@ def tile_attention_prop_pa_kernel(
         add_bias2(1, 1)
         squares(0, 2)
         leaky2(0, 3)
+        both_sums(0)
+        squares(0, 3)
         squares(1, 0)
         add_bias2(1, 3, True)
         leaky2(1, 1)
-        aggregate(0)
-        squares(0, 3)
-        squares(1, 1)
+        first_squares()
         leaky2(1, 2)
-        aggregate(1)
+        both_sums(1)
+        known(0)
+        squares(1, 1)
+        inverse_deviation(0)
         leaky2(1, 3)
+        both_sums(2)
+        known(1)
+        gain_and_shift(0)
         squares(1, 2)
+        inverse_deviation(1)
+        both_sums(3)
+        known(2)
+        gain_and_shift(1)
+        known(3)
         squares(1, 3)
-        aggregate(2)
-        aggregate(3)
-        gain_and_shift()
+        inverse_deviation(2)
+        inverse_deviation(3)
+        gain_and_shift(2)
+        gain_and_shift(3)
 
         on_scalar, on_vector = nc.scalar.copy, nc.vector.tensor_copy
         for q in range(4):

@@ -241,9 +241,9 @@ def tile_attention_prop_pa_kernel(
                 accum_out=square_sums[:, c, half : half + 1],
             )
 
-        def first_squares():
+        def first_squares(c):
             nc.vector.tensor_scalar(
-                out=first_part[:], in0=square_sums[:, :, 0], scalar1=1.0 / ROWS,
+                out=first_part[:, c : c + 1], in0=square_sums[:, c, 0:1], scalar1=1.0 / ROWS,
                 scalar2=EPS * HALF * HALF, op0=ALU.mult, op1=ALU.add,
             )
 
@@ -275,29 +275,34 @@ def tile_attention_prop_pa_kernel(
                 op0=ALU.mult, op1=ALU.add,
             )
 
-        QUARTER = ROWS // 4
-
-        def normalise(c, q, on_scalar=False):
-            if c == 0:
-                normed[q] = work.tile([P, FEAT_TILES, QUARTER], F32, name="normed")
-            rows = slice(QUARTER * q, QUARTER * (q + 1))
+        def normalise(c, b):
+            if b == 0:
+                normed[c] = work.tile([P, ROWS], F32, name="normed")
+            rows = slice(HALF * b, HALF * (b + 1))
             nc.vector.tensor_scalar(
-                out=normed[q][:, c, :], in0=h2[:, c, rows], scalar1=affine[:, c, 0:1],
+                out=normed[c][:, rows], in0=h2[:, c, rows], scalar1=affine[:, c, 0:1],
                 scalar2=affine[:, c, 1:2], op0=ALU.mult, op1=ALU.add,
             )
 
-        def flip_back(i):
-            back[i] = psum.tile([P, FEAT_TILES, P], F32, name="back", tag="bank")
-            for c in range(FEAT_TILES):
+        def flip_back(c, b):
+            back[c, b] = psum.tile([P, 4, P], F32, name="back", tag="bank")
+            for j in range(4):
+                i = 4 * b + j
                 nc.tensor.transpose(
-                    out=back[i][:, c, :], in_=normed[i // 2][:, c, P * (i % 2) : P * (i % 2 + 1)],
-                    identity=ident[:],
+                    out=back[c, b][:, j, :], in_=normed[c][:, P * i : P * (i + 1)], identity=ident[:]
                 )
 
-        def leave(i, copier):
-            copier(out=out_sb[:, i, :], in_=back[i][:].rearrange("p c m -> p (c m)"))
-            nc.sync.dma_start(out=out_rows[:, i, :], in_=out_sb[:, i, :])
+        def store(c, b, copier):
+            feats = slice(P * c, P * (c + 1))
+            tiles = slice(4 * b, 4 * (b + 1))
+            copier(out=out_sb[:, tiles, feats], in_=back[c, b][:])
+            nc.sync.dma_start(out=out_rows[:, tiles, feats], in_=out_sb[:, tiles, feats])
 
+        def norm(c):
+            gain_and_shift(c)
+            for b in range(2):
+                normalise(c, b)
+                flip_back(c, b)
 
         permute_w1()
         for g in range(2):
@@ -328,46 +333,45 @@ def tile_attention_prop_pa_kernel(
         leaky2(0, 1)
         leaky2(0, 2)
         squares(0, 1)
-        add_bias2(1, 2, True)
+        first_squares(0)
         leaky2(1, 0)
         add_bias2(1, 1)
-        squares(0, 2)
+        squares(1, 0)
         leaky2(0, 3)
         both_sums(0)
-        squares(0, 3)
-        squares(1, 0)
-        add_bias2(1, 3, True)
+        first_squares(1)
+        squares(0, 2)
         leaky2(1, 1)
-        first_squares()
-        leaky2(1, 2)
-        both_sums(1)
         known(0)
-        squares(1, 1)
+        add_bias2(1, 2)
         inverse_deviation(0)
-        leaky2(1, 3)
-        both_sums(2)
+        squares(1, 1)
+        both_sums(1)
+        first_squares(2)
+        squares(0, 3)
+        add_bias2(1, 3)
+        leaky2(1, 2)
         known(1)
-        gain_and_shift(0)
-        squares(1, 2)
+        norm(0)
         inverse_deviation(1)
-        both_sums(3)
+        squares(1, 2)
+        both_sums(2)
+        first_squares(3)
+        leaky2(1, 3)
         known(2)
-        gain_and_shift(1)
-        known(3)
-        squares(1, 3)
+        store(0, 0, nc.scalar.copy)
+        norm(1)
         inverse_deviation(2)
+        squares(1, 3)
+        both_sums(3)
+        store(0, 1, nc.vector.tensor_copy)
+        known(3)
+        norm(2)
         inverse_deviation(3)
-        gain_and_shift(2)
-        gain_and_shift(3)
-
-        on_scalar, on_vector = nc.scalar.copy, nc.vector.tensor_copy
-        for q in range(4):
-            for c in range(FEAT_TILES):
-                normalise(c, q)
-            flip_back(2 * q)
-            flip_back(2 * q + 1)
-            if q >= 1:
-                leave(2 * q - 2, on_scalar)
-                leave(2 * q - 1, on_scalar if q % 2 else on_vector)
-        leave(6, on_scalar)
-        leave(7, on_vector)
+        store(1, 0, nc.scalar.copy)
+        store(1, 1, nc.vector.tensor_copy)
+        norm(3)
+        store(2, 0, nc.scalar.copy)
+        store(2, 1, nc.vector.tensor_copy)
+        store(3, 0, nc.scalar.copy)
+        store(3, 1, nc.vector.tensor_copy)

@@ -18,9 +18,9 @@ ROWS = 1024
 FEAT = 512
 ROW_TILES = ROWS // P
 FEAT_TILES = FEAT // P
-PAIRS = ROW_TILES // 2
-HALVES = 2
-HALF = ROWS // HALVES
+PAIR = 2 * P
+PAIRS = ROWS // PAIR
+HALF = ROWS // 2
 WORDS = FEAT // 2
 EPS = 1e-5
 SLOPE = 0.01
@@ -46,6 +46,7 @@ def tile_attention_prop_pa_kernel(
         b1_bf = keep.tile([P, PACK], BF16)
         b1_cols = keep.tile([P, PACK], F32)
         vec_rows = keep.tile([P, P], BF16)
+        vec_cols = keep.tile([P, 3, FEAT_TILES], F32)
         ident = keep.tile([P, P], F32)
         ident_bf = keep.tile([P, P], BF16)
         x_codes = keep.tile([P, ROWS], U32, align_bytes=64)
@@ -53,27 +54,26 @@ def tile_attention_prop_pa_kernel(
         h_codes = keep.tile([P, ROWS], U32, align_bytes=64)
         h_plane = keep.tile([P, ROWS], U8, align_bytes=64)
         h2 = keep.tile([P, FEAT_TILES, ROWS], F32)
-        sums = keep.tile([P, FEAT_TILES, HALVES], F32)
-        square_sums = keep.tile([P, FEAT_TILES, HALVES], F32)
-        first_part = keep.tile([P, FEAT_TILES], F32)
-        neg_half_gamma = keep.tile([P, FEAT_TILES], F32)
-        offsets = keep.tile([P, FEAT_TILES, 2], F32)
-        stats = keep.tile([P, FEAT_TILES, 8], F32)
-        factors = keep.tile([P, FEAT_TILES, 2], F32)
-        affine = keep.tile([P, FEAT_TILES, 2], F32)
-        zero = keep.tile([P, 1], F32)
-        eps = keep.tile([P, 1], F32)
         out_sb = keep.tile([P, ROW_TILES, FEAT], F32)
+        sums = keep.tile([P, FEAT_TILES, 2], F32)
+        square_sums = keep.tile([P, FEAT_TILES, 2], F32)
+        first_part = keep.tile([P, FEAT_TILES], F32)
+        half_gap = keep.tile([P, FEAT_TILES], F32)
+        known_part = keep.tile([P, FEAT_TILES], F32)
+        inv_std = keep.tile([P, FEAT_TILES], F32)
+        neg_half_gamma = keep.tile([P, FEAT_TILES], F32)
+        factors = keep.tile([P, FEAT_TILES, 2], F32)
+        offsets = keep.tile([P, FEAT_TILES, 2], F32)
+        affine = keep.tile([P, FEAT_TILES, 2], F32)
+        one = keep.tile([P, 1], F32)
+        warm = keep.tile([P, 1], F32)
 
         nc.vector.memset(w_planes[:].rearrange("p w n -> p (w n)").bitcast(I32), 0)
-        one = keep.tile([P, 1], F32)
         nc.vector.memset(one[:], 1.0)
         nc.vector.memset(vec_rows[:], 0.0)
-        nc.vector.memset(zero[:], 0.0)
         nc.vector.memset(offsets[:], 0.0)
         make_identity(nc, ident[:])
         nc.vector.tensor_copy(out=ident_bf[:], in_=ident[:])
-        warm = keep.tile([P, 1], F32)
         nc.scalar.activation(out=warm[:], in_=one[:], func=ACT.Abs_reciprocal_sqrt)
 
         x_rows = x.rearrange("(p i) k -> p i k", i=ROW_TILES)
@@ -116,69 +116,72 @@ def tile_attention_prop_pa_kernel(
             )
             nc.vector.tensor_copy(out=b1_cols[:], in_=b1_bf[:])
 
-        grouped_x, grouped_h, acc1, biased = {}, {}, {}, {}
+        grouped_x, grouped_h, acc1, biased1 = {}, {}, {}, {}
 
-        def flip(word_columns, grouped):
-            flipped = psum.tile([P, 2, 2, P], F32, tag="bank")
-            for a in range(2):
-                for u in range(2):
-                    nc.tensor.transpose(out=flipped[:, a, u, :], in_=word_columns(a, u), identity=ident[:])
-            nc.scalar.copy(out=grouped[:].bitcast(F32), in_=flipped[:].rearrange("p a u r -> p a r u"))
-
-        def quantise(g, grouped, codes, plane):
-            cols = slice(2 * P * g, 2 * P * (g + 1))
-            nc.vector.quantize_mx(
-                out=codes[:, cols].bitcast(FP8X4),
-                scales=plane[:, cols],
-                in_=grouped[:].rearrange("p a r t -> p (a r t)"),
-            )
+        def columns(g):
+            return slice(PAIR * g, PAIR * (g + 1))
 
         def flip_x(g):
             grouped_x[g] = work.tile([P, 2, P, PACK], BF16, name="grouped_x", align_bytes=64)
             x_words = x_sb[:].bitcast(F32)
-            flip(lambda a, u: x_words[:, 2 * g + a, u:WORDS:2], grouped_x[g])
+            flipped = psum.tile([P, 2, 2, P], F32, tag="bank")
+            for a in range(2):
+                for u in range(2):
+                    nc.tensor.transpose(
+                        out=flipped[:, a, u, :], in_=x_words[:, 2 * g + a, u:WORDS:2], identity=ident[:]
+                    )
+            nc.scalar.copy(
+                out=grouped_x[g][:].bitcast(F32), in_=flipped[:].rearrange("p a u r -> p a r u")
+            )
+
+        def quantise_x(g):
+            nc.vector.quantize_mx(
+                out=x_codes[:, columns(g)].bitcast(FP8X4),
+                scales=x_plane[:, columns(g)],
+                in_=grouped_x[g][:].rearrange("p a r t -> p (a r t)"),
+            )
 
         def multiply1(g):
-            cols = slice(2 * P * g, 2 * P * (g + 1))
             for b in range(2):
-                acc1[g, b] = psum.tile([P, 2, 2 * P], F32, name="acc1", tag="bank")
+                bank = psum.tile([P, 2, PAIR], F32, name="acc1", tag="bank")
                 for s in range(2):
                     t = 2 * b + s
+                    acc1[g, t] = bank[:, s, :]
                     nc.tensor.matmul_mx(
-                        out=acc1[g, b][:, s, :],
+                        out=acc1[g, t],
                         lhsT=w1_codes[:, P * t : P * (t + 1)].bitcast(FP8X4),
                         lhsT_scale=w1_plane[:, P * t : P * (t + 1)],
-                        rhs=x_codes[:, cols].bitcast(FP8X4),
-                        rhs_scale=x_plane[:, cols],
+                        rhs=x_codes[:, columns(g)].bitcast(FP8X4),
+                        rhs_scale=x_plane[:, columns(g)],
                         start=True,
                         stop=True,
                     )
 
         def add_bias1(g):
-            biased[g] = work.tile([P, PACK, 2 * P], F32, name="biased")
+            biased1[g] = work.tile([P, PACK, PAIR], F32, name="biased1")
             for t in range(PACK):
                 nc.scalar.activation(
-                    out=biased[g][:, t, :], in_=acc1[g, t // 2][:, t % 2, :], func=ACT.Identity,
-                    bias=b1_cols[:, t : t + 1],
+                    out=biased1[g][:, t, :], in_=acc1[g, t], func=ACT.Identity, bias=b1_cols[:, t : t + 1]
                 )
 
         def leaky1(g):
-            grouped_h[g] = work.tile([P, 2 * P, PACK], BF16, name="grouped_h", align_bytes=64)
-            turned = biased[g][:].rearrange("p t r -> p r t")
+            grouped_h[g] = work.tile([P, PAIR, PACK], BF16, name="grouped_h", align_bytes=64)
+            turned = biased1[g][:].rearrange("p t r -> p r t")
             nc.vector.scalar_tensor_tensor(
-                out=grouped_h[g][:], in0=turned, scalar=SLOPE, in1=turned, op0=ALU.mult, op1=ALU.max,
+                out=grouped_h[g][:], in0=turned, scalar=SLOPE, in1=turned, op0=ALU.mult, op1=ALU.max
             )
 
         def quantise_h(g):
-            cols = slice(2 * P * g, 2 * P * (g + 1))
             nc.vector.quantize_mx(
-                out=h_codes[:, cols].bitcast(FP8X4),
-                scales=h_plane[:, cols],
+                out=h_codes[:, columns(g)].bitcast(FP8X4),
+                scales=h_plane[:, columns(g)],
                 in_=grouped_h[g][:].rearrange("p r t -> p (r t)"),
             )
 
-        vec_cols = keep.tile([P, 3, FEAT_TILES], F32)
         acc2, biased2 = {}, {}
+
+        def rows_of(j):
+            return slice(HALF * j, HALF * (j + 1))
 
         def spread_vectors():
             vec_ps = psum.tile([P, P], BF16, tag="bank")
@@ -192,122 +195,98 @@ def tile_attention_prop_pa_kernel(
             nc.scalar.activation(out=neg_half_gamma[:], in_=vec_cols[:, 1, :], func=ACT.Copy, scale=-0.5)
             nc.scalar.copy(out=offsets[:, :, 1], in_=vec_cols[:, 2, :])
 
-        def multiply2(half, c):
-            rows = slice(HALF * half, HALF * (half + 1))
-            acc2[half, c] = psum.tile([P, HALF], F32, name="acc2", tag="bank")
+        def multiply2(j, c):
+            acc2[j, c] = psum.tile([P, HALF], F32, name="acc2", tag="bank")
             nc.tensor.matmul_mx(
-                out=acc2[half, c][:],
+                out=acc2[j, c][:],
                 lhsT=w_bytes[:, 1, PACK * P * c : PACK * P * (c + 1)].bitcast(FP8X4),
                 lhsT_scale=w_planes[:, 1, P * c : P * (c + 1)],
-                rhs=h_codes[:, rows].bitcast(FP8X4),
-                rhs_scale=h_plane[:, rows],
+                rhs=h_codes[:, rows_of(j)].bitcast(FP8X4),
+                rhs_scale=h_plane[:, rows_of(j)],
                 start=True,
                 stop=True,
             )
 
-        def add_bias2(half, c, on_vector=False):
-            biased2[half, c] = work.tile([P, HALF], F32, name="biased2", bufs=8)
-            if on_vector:
-                nc.vector.tensor_scalar(
-                    out=biased2[half, c][:], in0=acc2[half, c][:], scalar1=vec_cols[:, 0, c : c + 1],
-                    scalar2=None, op0=ALU.add,
-                )
-            else:
-                nc.scalar.activation(
-                    out=biased2[half, c][:], in_=acc2[half, c][:], func=ACT.Identity,
-                    bias=vec_cols[:, 0, c : c + 1],
-                )
+        def add_bias2(j, c):
+            biased2[j, c] = work.tile([P, HALF], F32, name="biased2", bufs=2 * FEAT_TILES)
+            nc.scalar.activation(
+                out=biased2[j, c][:], in_=acc2[j, c][:], func=ACT.Identity, bias=vec_cols[:, 0, c : c + 1]
+            )
 
-        def leaky2(half, c):
+        def leaky2(j, c):
             nc.vector.scalar_tensor_tensor(
-                out=h2[:, c, HALF * half : HALF * (half + 1)],
-                in0=biased2[half, c][:], scalar=SLOPE, in1=biased2[half, c][:],
-                op0=ALU.mult, op1=ALU.max,
-                accum_out=sums[:, c, half : half + 1],
+                out=h2[:, c, rows_of(j)], in0=biased2[j, c][:], scalar=SLOPE, in1=biased2[j, c][:],
+                op0=ALU.mult, op1=ALU.max, accum_out=sums[:, c, j : j + 1],
             )
 
         normed, back = {}, {}
 
-        def stat(c, s):
-            return stats[:, c, s : s + 1]
+        def col(tile, c):
+            return tile[:, c : c + 1]
 
-        HALF_GAP, KNOWN, RSTD = range(3)
-
-        def squares(half, c):
+        def squares(j, c):
             unread = work.tile([P, HALF], BF16, name="unread")
             nc.scalar.activation(
-                out=unread[:], in_=h2[:, c, HALF * half : HALF * (half + 1)], func=ACT.Square,
-                scale=-float(HALF), bias=sums[:, c, half : half + 1],
-                accum_out=square_sums[:, c, half : half + 1],
+                out=unread[:], in_=h2[:, c, rows_of(j)], func=ACT.Square, scale=-float(HALF),
+                bias=sums[:, c, j : j + 1], accum_out=square_sums[:, c, j : j + 1],
             )
 
         def first_squares(c):
             nc.vector.tensor_scalar(
-                out=first_part[:, c : c + 1], in0=square_sums[:, c, 0:1], scalar1=1.0 / ROWS,
+                out=col(first_part, c), in0=square_sums[:, c, 0:1], scalar1=1.0 / ROWS,
                 scalar2=EPS * HALF * HALF, op0=ALU.mult, op1=ALU.add,
             )
 
         def both_sums(c):
             nc.vector.tensor_scalar(
-                out=stat(c, HALF_GAP), in0=sums[:, c, 1:2], scalar1=sums[:, c, 0:1], scalar2=0.5,
+                out=col(half_gap, c), in0=sums[:, c, 1:2], scalar1=sums[:, c, 0:1], scalar2=0.5,
                 op0=ALU.subtract, op1=ALU.mult,
             )
             nc.vector.tensor_scalar(
                 out=factors[:, c, 1:2], in0=sums[:, c, 1:2], scalar1=sums[:, c, 0:1],
-                scalar2=neg_half_gamma[:, c : c + 1], op0=ALU.add, op1=ALU.mult,
+                scalar2=col(neg_half_gamma, c), op0=ALU.add, op1=ALU.mult,
             )
 
         def known(c):
             nc.vector.tensor_scalar(
-                out=stat(c, KNOWN), in0=stat(c, HALF_GAP), scalar1=stat(c, HALF_GAP),
-                scalar2=first_part[:, c : c + 1], op0=ALU.mult, op1=ALU.add,
+                out=col(known_part, c), in0=col(half_gap, c), scalar1=col(half_gap, c),
+                scalar2=col(first_part, c), op0=ALU.mult, op1=ALU.add,
             )
 
         def inverse_deviation(c):
             nc.scalar.activation(
-                out=stat(c, RSTD), in_=square_sums[:, c, 1:2], func=ACT.Abs_reciprocal_sqrt,
-                scale=1.0 / ROWS, bias=stat(c, KNOWN),
+                out=col(inv_std, c), in_=square_sums[:, c, 1:2], func=ACT.Abs_reciprocal_sqrt,
+                scale=1.0 / ROWS, bias=col(known_part, c),
             )
 
-        def gain_and_shift(c):
+        def normalise(c):
             nc.vector.scalar_tensor_tensor(
-                out=affine[:, c, :], in0=factors[:, c, :], scalar=stat(c, RSTD), in1=offsets[:, c, :],
+                out=affine[:, c, :], in0=factors[:, c, :], scalar=col(inv_std, c), in1=offsets[:, c, :],
                 op0=ALU.mult, op1=ALU.add,
             )
-
-        def normalise(c, b):
-            if b == 0:
-                normed[c] = work.tile([P, ROWS], F32, name="normed")
-            rows = slice(HALF * b, HALF * (b + 1))
-            nc.vector.tensor_scalar(
-                out=normed[c][:, rows], in0=h2[:, c, rows], scalar1=affine[:, c, 0:1],
-                scalar2=affine[:, c, 1:2], op0=ALU.mult, op1=ALU.add,
-            )
-
-        def flip_back(c, b):
-            back[c, b] = psum.tile([P, 4, P], F32, name="back", tag="bank")
-            for j in range(4):
-                i = 4 * b + j
-                nc.tensor.transpose(
-                    out=back[c, b][:, j, :], in_=normed[c][:, P * i : P * (i + 1)], identity=ident[:]
+            normed[c] = work.tile([P, ROWS], F32, name="normed")
+            for j in range(2):
+                nc.vector.tensor_scalar(
+                    out=normed[c][:, rows_of(j)], in0=h2[:, c, rows_of(j)], scalar1=affine[:, c, 0:1],
+                    scalar2=affine[:, c, 1:2], op0=ALU.mult, op1=ALU.add,
                 )
+                back[c, j] = psum.tile([P, 4, P], F32, name="back", tag="bank")
+                for i in range(4):
+                    nc.tensor.transpose(
+                        out=back[c, j][:, i, :], in_=normed[c][:, P * (4 * j + i) : P * (4 * j + i + 1)],
+                        identity=ident[:],
+                    )
 
-        def store(c, b, copier):
+        def store(c, j, copy):
             feats = slice(P * c, P * (c + 1))
-            tiles = slice(4 * b, 4 * (b + 1))
-            copier(out=out_sb[:, tiles, feats], in_=back[c, b][:])
+            tiles = slice(4 * j, 4 * (j + 1))
+            copy(out=out_sb[:, tiles, feats], in_=back[c, j][:])
             nc.sync.dma_start(out=out_rows[:, tiles, feats], in_=out_sb[:, tiles, feats])
-
-        def norm(c):
-            gain_and_shift(c)
-            for b in range(2):
-                normalise(c, b)
-                flip_back(c, b)
 
         permute_w1()
         for g in range(2):
             flip_x(g)
-            quantise(g, grouped_x[g], x_codes, x_plane)
+            quantise_x(g)
         multiply1(0)
         for g in range(PAIRS):
             add_bias1(g)
@@ -317,7 +296,7 @@ def tile_attention_prop_pa_kernel(
                 multiply1(g + 1)
             leaky1(g)
             if g + 2 < PAIRS:
-                quantise(g + 2, grouped_x[g + 2], x_codes, x_plane)
+                quantise_x(g + 2)
             if g == PAIRS - 1:
                 spread_vectors()
                 for c in range(FEAT_TILES):
@@ -327,51 +306,36 @@ def tile_attention_prop_pa_kernel(
             quantise_h(g)
         for c in range(FEAT_TILES):
             multiply2(1, c)
-
-        squares(0, 0)
-        add_bias2(1, 0)
         leaky2(0, 1)
-        leaky2(0, 2)
-        squares(0, 1)
-        first_squares(0)
-        leaky2(1, 0)
-        add_bias2(1, 1)
-        squares(1, 0)
-        leaky2(0, 3)
-        both_sums(0)
-        first_squares(1)
-        squares(0, 2)
-        leaky2(1, 1)
-        known(0)
-        add_bias2(1, 2)
-        inverse_deviation(0)
-        squares(1, 1)
-        both_sums(1)
-        first_squares(2)
-        squares(0, 3)
-        add_bias2(1, 3)
-        leaky2(1, 2)
-        known(1)
-        norm(0)
-        inverse_deviation(1)
-        squares(1, 2)
-        both_sums(2)
-        first_squares(3)
-        leaky2(1, 3)
-        known(2)
-        store(0, 0, nc.scalar.copy)
-        norm(1)
-        inverse_deviation(2)
-        squares(1, 3)
-        both_sums(3)
-        store(0, 1, nc.vector.tensor_copy)
-        known(3)
-        norm(2)
-        inverse_deviation(3)
-        store(1, 0, nc.scalar.copy)
-        store(1, 1, nc.vector.tensor_copy)
-        norm(3)
-        store(2, 0, nc.scalar.copy)
-        store(2, 1, nc.vector.tensor_copy)
-        store(3, 0, nc.scalar.copy)
-        store(3, 1, nc.vector.tensor_copy)
+
+        AHEAD = 2
+        SUMS_LAG = 1
+        KNOWN_LAG = 2
+        NORM_LAG = 3
+        STORE_LAG = 4
+
+        def tiles_at(c):
+            return [c] if 0 <= c < FEAT_TILES else []
+
+        for step in range(FEAT_TILES + STORE_LAG):
+            for c in tiles_at(step):
+                squares(0, c)
+                add_bias2(1, c)
+            for c in tiles_at(step - KNOWN_LAG):
+                known(c)
+                inverse_deviation(c)
+            for c in tiles_at(step - STORE_LAG):
+                store(c, 0, nc.scalar.copy)
+            for c in tiles_at(step - NORM_LAG):
+                normalise(c)
+            for c in tiles_at(step + AHEAD):
+                leaky2(0, c)
+            for c in tiles_at(step - SUMS_LAG):
+                both_sums(c)
+            for c in tiles_at(step):
+                first_squares(c)
+                leaky2(1, c)
+            for c in tiles_at(step - SUMS_LAG):
+                squares(1, c)
+            for c in tiles_at(step - STORE_LAG):
+                store(c, 1, nc.vector.tensor_copy)

@@ -160,9 +160,16 @@ def tile_attention_prop_pa_kernel(
         def add_bias1(g):
             biased1[g] = work.tile([P, PACK, PAIR], F32, name="biased1")
             for t in range(PACK):
-                nc.scalar.activation(
-                    out=biased1[g][:, t, :], in_=acc1[g, t], func=ACT.Identity, bias=b1_cols[:, t : t + 1]
-                )
+                if g == 0 and t >= PACK // 2:
+                    nc.vector.tensor_scalar(
+                        out=biased1[g][:, t, :], in0=acc1[g, t], scalar1=b1_cols[:, t : t + 1],
+                        scalar2=None, op0=ALU.add,
+                    )
+                else:
+                    nc.scalar.activation(
+                        out=biased1[g][:, t, :], in_=acc1[g, t], func=ACT.Identity,
+                        bias=b1_cols[:, t : t + 1],
+                    )
 
         def leaky1(g):
             grouped_h[g] = work.tile([P, PAIR, PACK], BF16, name="grouped_h", align_bytes=64)
@@ -279,9 +286,11 @@ def tile_attention_prop_pa_kernel(
 
         def store(c, j, copy):
             feats = slice(P * c, P * (c + 1))
-            tiles = slice(4 * j, 4 * (j + 1))
-            copy(out=out_sb[:, tiles, feats], in_=back[c, j][:])
-            nc.sync.dma_start(out=out_rows[:, tiles, feats], in_=out_sb[:, tiles, feats])
+            piece = 2 if c == FEAT_TILES - 1 else 4
+            for i in range(0, 4, piece):
+                tiles = slice(4 * j + i, 4 * j + i + piece)
+                copy(out=out_sb[:, tiles, feats], in_=back[c, j][:, i : i + piece, :])
+                nc.sync.dma_start(out=out_rows[:, tiles, feats], in_=out_sb[:, tiles, feats])
 
         permute_w1()
         for g in range(2):

@@ -56,10 +56,10 @@ def tile_attention_prop_pa_kernel(
         h2 = keep.tile([P, FEAT_TILES, ROWS], F32)
         out_sb = keep.tile([P, ROW_TILES, FEAT], F32)
         sums = keep.tile([P, FEAT_TILES, 2], F32)
-        square_sums = keep.tile([P, FEAT_TILES, 2], F32)
-        first_part = keep.tile([P, FEAT_TILES], F32)
+        square_sums = keep.tile([P, FEAT_TILES], F32)
         half_gap = keep.tile([P, FEAT_TILES], F32)
         known_part = keep.tile([P, FEAT_TILES], F32)
+        scaled_b2 = keep.tile([P, FEAT_TILES], F32)
         inv_std = keep.tile([P, FEAT_TILES], F32)
         neg_half_gamma = keep.tile([P, FEAT_TILES], F32)
         factors = keep.tile([P, FEAT_TILES, 2], F32)
@@ -122,17 +122,23 @@ def tile_attention_prop_pa_kernel(
             return slice(PAIR * g, PAIR * (g + 1))
 
         def flip_x(g):
-            grouped_x[g] = work.tile([P, 2, P, PACK], BF16, name="grouped_x", align_bytes=64)
+            grouped_x[g] = work.tile([P, 2, P, PACK], BF16, name="grouped_x", bufs=PAIRS, align_bytes=64)
             x_words = x_sb[:].bitcast(F32)
-            flipped = psum.tile([P, 2, 2, P], F32, tag="bank")
-            for a in range(2):
-                for u in range(2):
-                    nc.tensor.transpose(
-                        out=flipped[:, a, u, :], in_=x_words[:, 2 * g + a, u:WORDS:2], identity=ident[:]
-                    )
-            nc.scalar.copy(
-                out=grouped_x[g][:].bitcast(F32), in_=flipped[:].rearrange("p a u r -> p a r u")
-            )
+            copies = ((0, 1, nc.scalar.copy), (1, 2, nc.vector.tensor_copy)) if g == 0 else ((0, 2, nc.scalar.copy),)
+            banks = []
+            for first, end, copy in copies:
+                flipped = psum.tile([P, 2, 2, P], F32, name="flipped", tag="bank")
+                banks.append(flipped)
+                for a in range(first, end):
+                    for u in range(2):
+                        nc.tensor.transpose(
+                            out=flipped[:, a, u, :], in_=x_words[:, 2 * g + a, u:WORDS:2], identity=ident[:]
+                        )
+            for flipped, (first, end, copy) in zip(banks, copies):
+                copy(
+                    out=grouped_x[g][:, first:end, :, :].bitcast(F32),
+                    in_=flipped[:, first:end, :, :].rearrange("p a u r -> p a r u"),
+                )
 
         def quantise_x(g):
             nc.vector.quantize_mx(
@@ -158,7 +164,7 @@ def tile_attention_prop_pa_kernel(
                     )
 
         def add_bias1(g):
-            biased1[g] = work.tile([P, PACK, PAIR], F32, name="biased1")
+            biased1[g] = work.tile([P, PACK, PAIR], F32, name="biased1", bufs=PAIRS)
             for t in range(PACK):
                 if g == 0 and t >= PACK // 2:
                     nc.vector.tensor_scalar(
@@ -172,7 +178,7 @@ def tile_attention_prop_pa_kernel(
                     )
 
         def leaky1(g):
-            grouped_h[g] = work.tile([P, PAIR, PACK], BF16, name="grouped_h", align_bytes=64)
+            grouped_h[g] = work.tile([P, PAIR, PACK], BF16, name="grouped_h", bufs=PAIRS, align_bytes=64)
             turned = biased1[g][:].rearrange("p t r -> p r t")
             nc.vector.scalar_tensor_tensor(
                 out=grouped_h[g][:], in0=turned, scalar=SLOPE, in1=turned, op0=ALU.mult, op1=ALU.max
@@ -200,6 +206,7 @@ def tile_attention_prop_pa_kernel(
                 out=factors[:, :, 0], in_=vec_cols[:, 1, :], func=ACT.Copy, scale=float(HALF)
             )
             nc.scalar.activation(out=neg_half_gamma[:], in_=vec_cols[:, 1, :], func=ACT.Copy, scale=-0.5)
+            nc.scalar.activation(out=scaled_b2[:], in_=vec_cols[:, 0, :], func=ACT.Copy, scale=SLOPE)
             nc.scalar.copy(out=offsets[:, :, 1], in_=vec_cols[:, 2, :])
 
         def multiply2(j, c):
@@ -217,13 +224,14 @@ def tile_attention_prop_pa_kernel(
         def add_bias2(j, c):
             biased2[j, c] = work.tile([P, HALF], F32, name="biased2", bufs=2 * FEAT_TILES)
             nc.scalar.activation(
-                out=biased2[j, c][:], in_=acc2[j, c][:], func=ACT.Identity, bias=vec_cols[:, 0, c : c + 1]
+                out=biased2[j, c][:], in_=acc2[j, c][:], func=ACT.Identity, scale=SLOPE,
+                bias=scaled_b2[:, c : c + 1],
             )
 
         def leaky2(j, c):
             nc.vector.scalar_tensor_tensor(
-                out=h2[:, c, rows_of(j)], in0=biased2[j, c][:], scalar=SLOPE, in1=biased2[j, c][:],
-                op0=ALU.mult, op1=ALU.max, accum_out=sums[:, c, j : j + 1],
+                out=h2[:, c, rows_of(j)], in0=acc2[j, c][:], scalar=vec_cols[:, 0, c : c + 1],
+                in1=biased2[j, c][:], op0=ALU.add, op1=ALU.max, accum_out=sums[:, c, j : j + 1],
             )
 
         normed, back = {}, {}
@@ -231,17 +239,11 @@ def tile_attention_prop_pa_kernel(
         def col(tile, c):
             return tile[:, c : c + 1]
 
-        def squares(j, c):
-            unread = work.tile([P, HALF], BF16, name="unread")
+        def squares(c):
+            unread = work.tile([P, ROWS], BF16, name="unread")
             nc.scalar.activation(
-                out=unread[:], in_=h2[:, c, rows_of(j)], func=ACT.Square, scale=-float(HALF),
-                bias=sums[:, c, j : j + 1], accum_out=square_sums[:, c, j : j + 1],
-            )
-
-        def first_squares(c):
-            nc.vector.tensor_scalar(
-                out=col(first_part, c), in0=square_sums[:, c, 0:1], scalar1=1.0 / ROWS,
-                scalar2=EPS * HALF * HALF, op0=ALU.mult, op1=ALU.add,
+                out=unread[:], in_=h2[:, c, :], func=ACT.Square, scale=-float(HALF),
+                bias=sums[:, c, 0:1], accum_out=col(square_sums, c),
             )
 
         def both_sums(c):
@@ -253,25 +255,25 @@ def tile_attention_prop_pa_kernel(
                 out=factors[:, c, 1:2], in0=sums[:, c, 1:2], scalar1=sums[:, c, 0:1],
                 scalar2=col(neg_half_gamma, c), op0=ALU.add, op1=ALU.mult,
             )
-
-        def known(c):
             nc.vector.tensor_scalar(
                 out=col(known_part, c), in0=col(half_gap, c), scalar1=col(half_gap, c),
-                scalar2=col(first_part, c), op0=ALU.mult, op1=ALU.add,
+                scalar2=EPS * HALF * HALF, op0=ALU.mult, op1=ALU.subtract,
             )
 
         def inverse_deviation(c):
             nc.scalar.activation(
-                out=col(inv_std, c), in_=square_sums[:, c, 1:2], func=ACT.Abs_reciprocal_sqrt,
-                scale=1.0 / ROWS, bias=col(known_part, c),
+                out=col(inv_std, c), in_=col(square_sums, c), func=ACT.Abs_reciprocal_sqrt,
+                scale=-1.0 / ROWS, bias=col(known_part, c),
             )
 
-        def normalise(c):
+        def gain(c):
             nc.vector.scalar_tensor_tensor(
                 out=affine[:, c, :], in0=factors[:, c, :], scalar=col(inv_std, c), in1=offsets[:, c, :],
                 op0=ALU.mult, op1=ALU.add,
             )
-            normed[c] = work.tile([P, ROWS], F32, name="normed")
+
+        def normalise(c):
+            normed[c] = work.tile([P, ROWS], F32, name="normed", bufs=FEAT_TILES)
             for j in range(2):
                 nc.vector.tensor_scalar(
                     out=normed[c][:, rows_of(j)], in0=h2[:, c, rows_of(j)], scalar1=affine[:, c, 0:1],
@@ -284,67 +286,60 @@ def tile_attention_prop_pa_kernel(
                         identity=ident[:],
                     )
 
-        def store(c, j, copy):
+        def store(c):
             feats = slice(P * c, P * (c + 1))
             piece = 2 if c == FEAT_TILES - 1 else 4
-            for i in range(0, 4, piece):
-                tiles = slice(4 * j + i, 4 * j + i + piece)
-                copy(out=out_sb[:, tiles, feats], in_=back[c, j][:, i : i + piece, :])
-                nc.sync.dma_start(out=out_rows[:, tiles, feats], in_=out_sb[:, tiles, feats])
+            for j, copy in enumerate((nc.scalar.copy, nc.vector.tensor_copy)):
+                for i in range(0, 4, piece):
+                    tiles = slice(4 * j + i, 4 * j + i + piece)
+                    copy(out=out_sb[:, tiles, feats], in_=back[c, j][:, i : i + piece, :])
+                    nc.sync.dma_start(out=out_rows[:, tiles, feats], in_=out_sb[:, tiles, feats])
 
         permute_w1()
-        for g in range(2):
-            flip_x(g)
-            quantise_x(g)
+        flip_x(0)
+        quantise_x(0)
+        flip_x(1)
         multiply1(0)
-        for g in range(PAIRS):
-            add_bias1(g)
-            if g + 2 < PAIRS:
-                flip_x(g + 2)
-            if g + 1 < PAIRS:
-                multiply1(g + 1)
-            leaky1(g)
-            if g + 2 < PAIRS:
-                quantise_x(g + 2)
-            if g == PAIRS - 1:
-                spread_vectors()
-                for c in range(FEAT_TILES):
-                    multiply2(0, c)
-                    add_bias2(0, c)
-                leaky2(0, 0)
-            quantise_h(g)
+        add_bias1(0)
+        quantise_x(1)
+        flip_x(2)
+        flip_x(3)
+        multiply1(1)
+        leaky1(0)
+        add_bias1(1)
+        quantise_x(2)
+        quantise_x(3)
+        multiply1(2)
+        leaky1(1)
+        quantise_h(0)
+        quantise_h(1)
+        add_bias1(2)
+        multiply1(3)
+        add_bias1(3)
+        spread_vectors()
+        leaky1(2)
+        for c in range(FEAT_TILES):
+            multiply2(0, c)
+            add_bias2(0, c)
+        leaky1(3)
+        quantise_h(2)
+        quantise_h(3)
         for c in range(FEAT_TILES):
             multiply2(1, c)
-        leaky2(0, 1)
 
-        AHEAD = 2
-        SUMS_LAG = 1
-        KNOWN_LAG = 2
-        NORM_LAG = 3
-        STORE_LAG = 4
-
-        def tiles_at(c):
-            return [c] if 0 <= c < FEAT_TILES else []
-
-        for step in range(FEAT_TILES + STORE_LAG):
-            for c in tiles_at(step):
-                squares(0, c)
-                add_bias2(1, c)
-            for c in tiles_at(step - KNOWN_LAG):
-                known(c)
-                inverse_deviation(c)
-            for c in tiles_at(step - STORE_LAG):
-                store(c, 0, nc.scalar.copy)
-            for c in tiles_at(step - NORM_LAG):
-                normalise(c)
-            for c in tiles_at(step + AHEAD):
-                leaky2(0, c)
-            for c in tiles_at(step - SUMS_LAG):
-                both_sums(c)
-            for c in tiles_at(step):
-                first_squares(c)
-                leaky2(1, c)
-            for c in tiles_at(step - SUMS_LAG):
-                squares(1, c)
-            for c in tiles_at(step - STORE_LAG):
-                store(c, 1, nc.vector.tensor_copy)
+        stages = (
+            (lambda c: add_bias2(1, c), -3),
+            (squares, 2),
+            (inverse_deviation, 3),
+            (lambda c: leaky2(0, c), -6),
+            (lambda c: leaky2(1, c), -1),
+            (both_sums, 2),
+            (gain, 3),
+            (normalise, 4),
+            (store, 6),
+        )
+        for tick in range(-6, 2 * FEAT_TILES + 6):
+            for stage, lag in stages:
+                c, odd = divmod(tick - lag, 2)
+                if not odd and 0 <= c < FEAT_TILES:
+                    stage(c)

@@ -49,6 +49,7 @@ def tile_attention_prop_pa_kernel(
         vec_cols = keep.tile([P, 3, FEAT_TILES], F32)
         ident = keep.tile([P, P], F32)
         ident_bf = keep.tile([P, P], BF16)
+        zeros = keep.tile([P, FEAT], BF16)
         x_codes = keep.tile([P, ROWS], U32, align_bytes=64)
         x_plane = keep.tile([P, ROWS], U8, align_bytes=64)
         h_codes = keep.tile([P, ROWS], U32, align_bytes=64)
@@ -68,6 +69,7 @@ def tile_attention_prop_pa_kernel(
         one = keep.tile([P, 1], F32)
         warm = keep.tile([P, 1], F32)
 
+        nc.vector.memset(zeros[:].bitcast(I32), 0)
         nc.vector.memset(w_planes[:].rearrange("p w n -> p (w n)").bitcast(I32), 0)
         nc.vector.memset(one[:], 1.0)
         nc.vector.memset(vec_rows[:], 0.0)
@@ -295,8 +297,15 @@ def tile_attention_prop_pa_kernel(
                     copy(out=out_sb[:, tiles, feats], in_=back[c, j][:, i : i + piece, :])
                     nc.sync.dma_start(out=out_rows[:, tiles, feats], in_=out_sb[:, tiles, feats])
 
+        def keep_clock(matmuls):
+            unread_ps = psum.tile([P, FEAT], F32, tag="bank")
+            for m in range(matmuls):
+                nc.tensor.matmul(out=unread_ps[:], lhsT=zeros[:, 0:P], rhs=zeros[:], start=True, stop=True)
+
+        keep_clock(4)
         permute_w1()
         flip_x(0)
+        keep_clock(2)
         quantise_x(0)
         flip_x(1)
         multiply1(0)

@@ -69,7 +69,7 @@ def tile_attention_prop_pa_kernel(
         one = keep.tile([P, 1], F32)
         warm = keep.tile([P, 1], F32)
 
-        nc.vector.memset(zeros[:].bitcast(I32), 0)
+        nc.gpsimd.memset(zeros[:].bitcast(I32), 0)
         nc.vector.memset(w_planes[:].rearrange("p w n -> p (w n)").bitcast(I32), 0)
         nc.vector.memset(one[:], 1.0)
         nc.vector.memset(vec_rows[:], 0.0)
@@ -112,6 +112,8 @@ def tile_attention_prop_pa_kernel(
                 out=w1_plane[:].rearrange("p (t m) -> p t m", t=PACK),
                 in_=w_planes[:, 0, :].rearrange("p (m t) -> p t m", t=PACK),
             )
+
+        def permute_w1_words():
             nc.vector.tensor_copy(
                 out=w1_codes[:].rearrange("p (t m) -> p t m", t=PACK),
                 in_=w_bytes[:, 0, :].bitcast(I32).rearrange("p (m t) -> p t m", t=PACK),
@@ -225,6 +227,12 @@ def tile_attention_prop_pa_kernel(
 
         def add_bias2(j, c):
             biased2[j, c] = work.tile([P, HALF], F32, name="biased2", bufs=2 * FEAT_TILES)
+            if (j, c) == (1, FEAT_TILES - 1):
+                nc.vector.tensor_scalar(
+                    out=biased2[j, c][:], in0=acc2[j, c][:], scalar1=SLOPE,
+                    scalar2=scaled_b2[:, c : c + 1], op0=ALU.mult, op1=ALU.add,
+                )
+                return
             nc.scalar.activation(
                 out=biased2[j, c][:], in_=acc2[j, c][:], func=ACT.Identity, scale=SLOPE,
                 bias=scaled_b2[:, c : c + 1],
@@ -257,6 +265,8 @@ def tile_attention_prop_pa_kernel(
                 out=factors[:, c, 1:2], in0=sums[:, c, 1:2], scalar1=sums[:, c, 0:1],
                 scalar2=col(neg_half_gamma, c), op0=ALU.add, op1=ALU.mult,
             )
+
+        def known(c):
             nc.vector.tensor_scalar(
                 out=col(known_part, c), in0=col(half_gap, c), scalar1=col(half_gap, c),
                 scalar2=EPS * HALF * HALF, op0=ALU.mult, op1=ALU.subtract,
@@ -305,6 +315,7 @@ def tile_attention_prop_pa_kernel(
         keep_clock(4)
         permute_w1()
         flip_x(0)
+        permute_w1_words()
         keep_clock(2)
         quantise_x(0)
         flip_x(1)
@@ -340,14 +351,15 @@ def tile_attention_prop_pa_kernel(
             (lambda c: add_bias2(1, c), -3),
             (squares, 2),
             (inverse_deviation, 3),
-            (lambda c: leaky2(0, c), -6),
-            (lambda c: leaky2(1, c), -1),
-            (both_sums, 2),
+            (lambda c: leaky2(0, c), -5),
+            (lambda c: leaky2(1, c), 0),
+            (both_sums, 1),
+            (known, 2),
             (gain, 3),
             (normalise, 4),
             (store, 6),
         )
-        for tick in range(-6, 2 * FEAT_TILES + 6):
+        for tick in range(-5, 2 * FEAT_TILES + 6):
             for stage, lag in stages:
                 c, odd = divmod(tick - lag, 2)
                 if not odd and 0 <= c < FEAT_TILES:

@@ -36,7 +36,8 @@ def tile_attention_prop_pa_kernel(
         ctx.enter_context(tc.manual_schedule())
         keep = ctx.enter_context(tc.tile_pool(name="keep", bufs=1))
         work = ctx.enter_context(tc.tile_pool(name="work", bufs=3))
-        psum = ctx.enter_context(tc.psum_pool(name="psum", bufs=8))
+        psum = ctx.enter_context(tc.psum_pool(name="psum", bufs=7))
+        unread_psum = ctx.enter_context(tc.psum_pool(name="unread", bufs=1))
 
         x_sb = keep.tile([P, ROW_TILES, FEAT], BF16)
         w_bytes = keep.tile([P, 2, PACK * FEAT], U8, align_bytes=64)
@@ -49,7 +50,7 @@ def tile_attention_prop_pa_kernel(
         vec_cols = keep.tile([P, 3, FEAT_TILES], F32)
         ident = keep.tile([P, P], F32)
         ident_bf = keep.tile([P, P], BF16)
-        zeros = keep.tile([P, FEAT], BF16)
+        zeros = keep.tile([P, P], F32)
         x_codes = keep.tile([P, ROWS], U32, align_bytes=64)
         x_plane = keep.tile([P, ROWS], U8, align_bytes=64)
         h_codes = keep.tile([P, ROWS], U32, align_bytes=64)
@@ -301,16 +302,18 @@ def tile_attention_prop_pa_kernel(
         def store(c):
             feats = slice(P * c, P * (c + 1))
             piece = 2 if c == FEAT_TILES - 1 else 4
-            for j, copy in enumerate((nc.scalar.copy, nc.vector.tensor_copy)):
+            for j in range(2):
+                copy = nc.vector.tensor_copy if j == 1 and c != 2 else nc.scalar.copy
                 for i in range(0, 4, piece):
                     tiles = slice(4 * j + i, 4 * j + i + piece)
                     copy(out=out_sb[:, tiles, feats], in_=back[c, j][:, i : i + piece, :])
                     nc.sync.dma_start(out=out_rows[:, tiles, feats], in_=out_sb[:, tiles, feats])
 
+        unread_ps = unread_psum.tile([P, FEAT], F32)
+
         def keep_clock(matmuls):
-            unread_ps = psum.tile([P, FEAT], F32, tag="bank")
             for m in range(matmuls):
-                nc.tensor.matmul(out=unread_ps[:], lhsT=zeros[:, 0:P], rhs=zeros[:], start=True, stop=True)
+                nc.tensor.matmul(out=unread_ps[:, 0:P], lhsT=zeros[:], rhs=zeros[:], start=True, stop=True)
 
         keep_clock(4)
         permute_w1()
@@ -325,16 +328,19 @@ def tile_attention_prop_pa_kernel(
         flip_x(2)
         flip_x(3)
         multiply1(1)
+        keep_clock(1)
         leaky1(0)
         add_bias1(1)
         quantise_x(2)
         quantise_x(3)
         multiply1(2)
+        keep_clock(1)
         leaky1(1)
         quantise_h(0)
         quantise_h(1)
         add_bias1(2)
         multiply1(3)
+        keep_clock(1)
         add_bias1(3)
         spread_vectors()
         leaky1(2)
@@ -344,16 +350,26 @@ def tile_attention_prop_pa_kernel(
         leaky1(3)
         quantise_h(2)
         quantise_h(3)
-        for c in range(FEAT_TILES):
+        def keep_clock2(c):
+            for m in range(2):
+                nc.tensor.matmul(
+                    out=unread_ps[:, P * m : P * (m + 1)], lhsT=h2[:, c, HALF : HALF + P],
+                    rhs=h2[:, c, ROWS - P : ROWS], start=True, stop=True,
+                )
+
+        for c in range(FEAT_TILES - 1):
             multiply2(1, c)
+        leaky2(0, 0)
+        multiply2(1, FEAT_TILES - 1)
 
         stages = (
             (lambda c: add_bias2(1, c), -3),
             (squares, 2),
             (inverse_deviation, 3),
-            (lambda c: leaky2(0, c), -5),
+            (lambda c: leaky2(0, c) if c else None, -5),
             (lambda c: leaky2(1, c), 0),
             (both_sums, 1),
+            (keep_clock2, 1),
             (known, 2),
             (gain, 3),
             (normalise, 4),

@@ -288,7 +288,8 @@ def tile_attention_prop_pa_kernel(
         def normalise(c):
             normed[c] = work.tile([P, ROWS], F32, name="normed", bufs=FEAT_TILES)
             for j in range(2):
-                nc.vector.tensor_scalar(
+                engine = nc.gpsimd if c == 1 else nc.vector
+                engine.tensor_scalar(
                     out=normed[c][:, rows_of(j)], in0=h2[:, c, rows_of(j)], scalar1=affine[:, c, 0:1],
                     scalar2=affine[:, c, 1:2], op0=ALU.mult, op1=ALU.add,
                 )
@@ -303,7 +304,7 @@ def tile_attention_prop_pa_kernel(
             feats = slice(P * c, P * (c + 1))
             piece = 2 if c == FEAT_TILES - 1 else 4
             for j in range(2):
-                copy = nc.vector.tensor_copy if j == 1 and c != 2 else nc.scalar.copy
+                copy = nc.vector.tensor_copy if c == 0 or (j == 1 and c != 2) else nc.scalar.copy
                 for i in range(0, 4, piece):
                     tiles = slice(4 * j + i, 4 * j + i + piece)
                     copy(out=out_sb[:, tiles, feats], in_=back[c, j][:, i : i + piece, :])

from contextlib import ExitStack

import concourse.mybir as mybir
from concourse.masks import make_identity

F32 = mybir.dt.float32
BF16 = mybir.dt.bfloat16
I32 = mybir.dt.int32
U32 = mybir.dt.uint32
U8 = mybir.dt.uint8
FP8X4 = mybir.dt.float8_e4m3fn_x4
ALU = mybir.AluOpType
ACT = mybir.ActivationFunctionType

P = 128
PACK = 4
ROWS = 1024
FEAT = 512
ROW_TILES = ROWS // P
FEAT_TILES = FEAT // P
PAIR = 2 * P
PAIRS = ROWS // PAIR
HALF = ROWS // 2
WORDS = FEAT // 2
EPS = 1e-5
SLOPE = 0.01

FLOPS = 2 * 2 * ROWS * FEAT * FEAT


def tile_attention_prop_pa_kernel(
    tc, x, w1_words, w1_scales, b1, w2_words, w2_scales, b2, gamma, beta, out
):
    nc = tc.nc
    with ExitStack() as ctx:
        ctx.enter_context(tc.manual_schedule())
        keep = ctx.enter_context(tc.tile_pool(name="keep", bufs=1))
        work = ctx.enter_context(tc.tile_pool(name="work", bufs=3))
        psum = ctx.enter_context(tc.psum_pool(name="psum", bufs=7))
        unread_psum = ctx.enter_context(tc.psum_pool(name="unread", bufs=1))

        x_sb = keep.tile([P, ROW_TILES, FEAT], BF16)
        w_bytes = keep.tile([P, 2, PACK * FEAT], U8, align_bytes=64)
        w_planes = keep.tile([P, 2, FEAT], U8, align_bytes=64)
        w1_codes = keep.tile([P, FEAT], I32, align_bytes=64)
        w1_plane = keep.tile([P, FEAT], U8, align_bytes=64)
        b1_bf = keep.tile([P, PACK], BF16)
        b1_cols = keep.tile([P, PACK], F32)
        vec_rows = keep.tile([P, P], BF16)
        vec_cols = keep.tile([P, 3, FEAT_TILES], F32)
        ident = keep.tile([P, P], F32)
        ident_bf = keep.tile([P, P], BF16)
        zeros = keep.tile([P, P], F32)
        x_codes = keep.tile([P, ROWS], U32, align_bytes=64)
        x_plane = keep.tile([P, ROWS], U8, align_bytes=64)
        h_codes = keep.tile([P, ROWS], U32, align_bytes=64)
        h_plane = keep.tile([P, ROWS], U8, align_bytes=64)
        h2 = keep.tile([P, FEAT_TILES, ROWS], F32)
        out_sb = keep.tile([P, ROW_TILES, FEAT], F32)
        sums = keep.tile([P, FEAT_TILES, 2], F32)
        square_sums = keep.tile([P, FEAT_TILES], F32)
        half_gap = keep.tile([P, FEAT_TILES], F32)
        known_part = keep.tile([P, FEAT_TILES], F32)
        scaled_b2 = keep.tile([P, FEAT_TILES], F32)
        inv_std = keep.tile([P, FEAT_TILES], F32)
        neg_half_gamma = keep.tile([P, FEAT_TILES], F32)
        factors = keep.tile([P, FEAT_TILES, 2], F32)
        offsets = keep.tile([P, FEAT_TILES, 2], F32)
        affine = keep.tile([P, FEAT_TILES, 2], F32)
        one = keep.tile([P, 1], F32)
        warm = keep.tile([P, 1], F32)

        nc.gpsimd.memset(zeros[:].bitcast(I32), 0)
        nc.vector.memset(w_planes[:].rearrange("p w n -> p (w n)").bitcast(I32), 0)
        nc.vector.memset(one[:], 1.0)
        nc.vector.memset(vec_rows[:], 0.0)
        nc.vector.memset(offsets[:], 0.0)
        make_identity(nc, ident[:])
        nc.vector.tensor_copy(out=ident_bf[:], in_=ident[:])
        nc.scalar.activation(out=warm[:], in_=one[:], func=ACT.Abs_reciprocal_sqrt)

        x_rows = x.rearrange("(p i) k -> p i k", i=ROW_TILES)
        out_rows = out.rearrange("(p i) f -> p i f", i=ROW_TILES)

        def load_x(g):
            nc.sync.dma_start(out=x_sb[:, 2 * g : 2 * g + 2, :], in_=x_rows[:, 2 * g : 2 * g + 2, :])

        def load_weight(w, words, scales):
            for quad in range(4):
                nc.sync.dma_start(
                    out=w_planes[32 * quad : 32 * quad + 4, w, :].bitcast(I32),
                    in_=scales[0, 4 * quad : 4 * quad + 4, :].bitcast(I32),
                )
            nc.sync.dma_start(
                out=w_bytes[:, w, :].bitcast(I32),
                in_=words[0].rearrange("p n t -> p (n t)").bitcast(I32),
            )

        load_x(0)
        load_weight(0, w1_words, w1_scales)
        nc.sync.dma_start(out=b1_bf[:], in_=b1.rearrange("(p t) -> p t", t=PACK))
        for g in range(1, PAIRS):
            load_x(g)
        load_weight(1, w2_words, w2_scales)
        for v, vec in enumerate((b2, gamma, beta)):
            nc.sync.dma_start(
                out=vec_rows[FEAT_TILES * v : FEAT_TILES * (v + 1), :],
                in_=vec.rearrange("(c m) -> c m", m=P),
            )

        def permute_w1():
            nc.vector.tensor_copy(
                out=w1_plane[:].rearrange("p (t m) -> p t m", t=PACK),
                in_=w_planes[:, 0, :].rearrange("p (m t) -> p t m", t=PACK),
            )

        def permute_w1_words():
            nc.vector.tensor_copy(
                out=w1_codes[:].rearrange("p (t m) -> p t m", t=PACK),
                in_=w_bytes[:, 0, :].bitcast(I32).rearrange("p (m t) -> p t m", t=PACK),
            )
            nc.vector.tensor_copy(out=b1_cols[:], in_=b1_bf[:])

        grouped_x, grouped_h, acc1, biased1 = {}, {}, {}, {}

        def columns(g):
            return slice(PAIR * g, PAIR * (g + 1))

        def flip_x(g):
            grouped_x[g] = work.tile([P, 2, P, PACK], BF16, name="grouped_x", bufs=PAIRS, align_bytes=64)
            x_words = x_sb[:].bitcast(F32)
            copies = ((0, 1, nc.scalar.copy), (1, 2, nc.vector.tensor_copy)) if g == 0 else ((0, 2, nc.scalar.copy),)
            banks = []
            for first, end, copy in copies:
                flipped = psum.tile([P, 2, 2, P], F32, name="flipped", tag="bank")
                banks.append(flipped)
                for a in range(first, end):
                    for u in range(2):
                        nc.tensor.transpose(
                            out=flipped[:, a, u, :], in_=x_words[:, 2 * g + a, u:WORDS:2], identity=ident[:]
                        )
            for flipped, (first, end, copy) in zip(banks, copies):
                copy(
                    out=grouped_x[g][:, first:end, :, :].bitcast(F32),
                    in_=flipped[:, first:end, :, :].rearrange("p a u r -> p a r u"),
                )

        def quantise_x(g):
            nc.vector.quantize_mx(
                out=x_codes[:, columns(g)].bitcast(FP8X4),
                scales=x_plane[:, columns(g)],
                in_=grouped_x[g][:].rearrange("p a r t -> p (a r t)"),
            )

        def multiply1(g):
            for b in range(2):
                bank = psum.tile([P, 2, PAIR], F32, name="acc1", tag="bank")
                for s in range(2):
                    t = 2 * b + s
                    acc1[g, t] = bank[:, s, :]
                    nc.tensor.matmul_mx(
                        out=acc1[g, t],
                        lhsT=w1_codes[:, P * t : P * (t + 1)].bitcast(FP8X4),
                        lhsT_scale=w1_plane[:, P * t : P * (t + 1)],
                        rhs=x_codes[:, columns(g)].bitcast(FP8X4),
                        rhs_scale=x_plane[:, columns(g)],
                        start=True,
                        stop=True,
                    )

        def add_bias1(g):
            biased1[g] = work.tile([P, PACK, PAIR], F32, name="biased1", bufs=PAIRS)
            for t in range(PACK):
                if g == 0 and t >= PACK // 2:
                    nc.vector.tensor_scalar(
                        out=biased1[g][:, t, :], in0=acc1[g, t], scalar1=b1_cols[:, t : t + 1],
                        scalar2=None, op0=ALU.add,
                    )
                else:
                    nc.scalar.activation(
                        out=biased1[g][:, t, :], in_=acc1[g, t], func=ACT.Identity,
                        bias=b1_cols[:, t : t + 1],
                    )

        def leaky1(g):
            grouped_h[g] = work.tile([P, PAIR, PACK], BF16, name="grouped_h", bufs=PAIRS, align_bytes=64)
            turned = biased1[g][:].rearrange("p t r -> p r t")
            nc.vector.scalar_tensor_tensor(
                out=grouped_h[g][:], in0=turned, scalar=SLOPE, in1=turned, op0=ALU.mult, op1=ALU.max
            )

        def quantise_h(g):
            nc.vector.quantize_mx(
                out=h_codes[:, columns(g)].bitcast(FP8X4),
                scales=h_plane[:, columns(g)],
                in_=grouped_h[g][:].rearrange("p r t -> p (r t)"),
            )

        acc2, biased2 = {}, {}

        def rows_of(j):
            return slice(HALF * j, HALF * (j + 1))

        def spread_vectors():
            vec_ps = psum.tile([P, P], BF16, tag="bank")
            nc.tensor.transpose(out=vec_ps[:], in_=vec_rows[:], identity=ident_bf[:])
            nc.scalar.copy(
                out=vec_cols[:].rearrange("p v c -> p (v c)"), in_=vec_ps[:, 0 : 3 * FEAT_TILES]
            )
            nc.scalar.activation(
                out=factors[:, :, 0], in_=vec_cols[:, 1, :], func=ACT.Copy, scale=float(HALF)
            )
            nc.scalar.activation(out=neg_half_gamma[:], in_=vec_cols[:, 1, :], func=ACT.Copy, scale=-0.5)
            nc.scalar.activation(out=scaled_b2[:], in_=vec_cols[:, 0, :], func=ACT.Copy, scale=SLOPE)
            nc.scalar.copy(out=offsets[:, :, 1], in_=vec_cols[:, 2, :])

        def multiply2(j, c):
            acc2[j, c] = psum.tile([P, HALF], F32, name="acc2", tag="bank")
            nc.tensor.matmul_mx(
                out=acc2[j, c][:],
                lhsT=w_bytes[:, 1, PACK * P * c : PACK * P * (c + 1)].bitcast(FP8X4),
                lhsT_scale=w_planes[:, 1, P * c : P * (c + 1)],
                rhs=h_codes[:, rows_of(j)].bitcast(FP8X4),
                rhs_scale=h_plane[:, rows_of(j)],
                start=True,
                stop=True,
            )

        def add_bias2(j, c):
            biased2[j, c] = work.tile([P, HALF], F32, name="biased2", bufs=2 * FEAT_TILES)
            if (j, c) == (1, FEAT_TILES - 1):
                nc.vector.tensor_scalar(
                    out=biased2[j, c][:], in0=acc2[j, c][:], scalar1=SLOPE,
                    scalar2=scaled_b2[:, c : c + 1], op0=ALU.mult, op1=ALU.add,
                )
                return
            nc.scalar.activation(
                out=biased2[j, c][:], in_=acc2[j, c][:], func=ACT.Identity, scale=SLOPE,
                bias=scaled_b2[:, c : c + 1],
            )

        def leaky2(j, c):
            nc.vector.scalar_tensor_tensor(
                out=h2[:, c, rows_of(j)], in0=acc2[j, c][:], scalar=vec_cols[:, 0, c : c + 1],
                in1=biased2[j, c][:], op0=ALU.add, op1=ALU.max, accum_out=sums[:, c, j : j + 1],
            )

        normed, back = {}, {}

        def col(tile, c):
            return tile[:, c : c + 1]

        def squares(c):
            unread = work.tile([P, ROWS], BF16, name="unread")
            nc.scalar.activation(
                out=unread[:], in_=h2[:, c, :], func=ACT.Square, scale=-float(HALF),
                bias=sums[:, c, 0:1], accum_out=col(square_sums, c),
            )

        def both_sums(c):
            nc.vector.tensor_scalar(
                out=col(half_gap, c), in0=sums[:, c, 1:2], scalar1=sums[:, c, 0:1], scalar2=0.5,
                op0=ALU.subtract, op1=ALU.mult,
            )
            nc.vector.tensor_scalar(
                out=factors[:, c, 1:2], in0=sums[:, c, 1:2], scalar1=sums[:, c, 0:1],
                scalar2=col(neg_half_gamma, c), op0=ALU.add, op1=ALU.mult,
            )

        def known(c):
            nc.vector.tensor_scalar(
                out=col(known_part, c), in0=col(half_gap, c), scalar1=col(half_gap, c),
                scalar2=EPS * HALF * HALF, op0=ALU.mult, op1=ALU.subtract,
            )

        def inverse_deviation(c):
            nc.scalar.activation(
                out=col(inv_std, c), in_=col(square_sums, c), func=ACT.Abs_reciprocal_sqrt,
                scale=-1.0 / ROWS, bias=col(known_part, c),
            )

        def gain(c):
            nc.vector.scalar_tensor_tensor(
                out=affine[:, c, :], in0=factors[:, c, :], scalar=col(inv_std, c), in1=offsets[:, c, :],
                op0=ALU.mult, op1=ALU.add,
            )

        def normalise(c):
            normed[c] = work.tile([P, ROWS], F32, name="normed", bufs=FEAT_TILES)
            for j in range(2):
                engine = nc.gpsimd if c == 1 else nc.vector
                engine.tensor_scalar(
                    out=normed[c][:, rows_of(j)], in0=h2[:, c, rows_of(j)], scalar1=affine[:, c, 0:1],
                    scalar2=affine[:, c, 1:2], op0=ALU.mult, op1=ALU.add,
                )
                back[c, j] = psum.tile([P, 4, P], F32, name="back", tag="bank")
                for i in range(4):
                    nc.tensor.transpose(
                        out=back[c, j][:, i, :], in_=normed[c][:, P * (4 * j + i) : P * (4 * j + i + 1)],
                        identity=ident[:],
                    )

        def store(c):
            feats = slice(P * c, P * (c + 1))
            piece = 2 if c == FEAT_TILES - 1 else 4
            for j in range(2):
                copy = nc.vector.tensor_copy if c == 0 or (j == 1 and c != 2) else nc.scalar.copy
                for i in range(0, 4, piece):
                    tiles = slice(4 * j + i, 4 * j + i + piece)
                    copy(out=out_sb[:, tiles, feats], in_=back[c, j][:, i : i + piece, :])
                    nc.sync.dma_start(out=out_rows[:, tiles, feats], in_=out_sb[:, tiles, feats])

        unread_ps = unread_psum.tile([P, FEAT], F32)

        def keep_clock(matmuls):
            for m in range(matmuls):
                nc.tensor.matmul(out=unread_ps[:, 0:P], lhsT=zeros[:], rhs=zeros[:], start=True, stop=True)

        keep_clock(4)
        permute_w1()
        flip_x(0)
        permute_w1_words()
        keep_clock(2)
        quantise_x(0)
        flip_x(1)
        multiply1(0)
        add_bias1(0)
        quantise_x(1)
        flip_x(2)
        flip_x(3)
        multiply1(1)
        keep_clock(1)
        leaky1(0)
        add_bias1(1)
        quantise_x(2)
        quantise_x(3)
        multiply1(2)
        keep_clock(1)
        leaky1(1)
        quantise_h(0)
        quantise_h(1)
        add_bias1(2)
        multiply1(3)
        keep_clock(1)
        add_bias1(3)
        spread_vectors()
        leaky1(2)
        for c in range(FEAT_TILES):
            multiply2(0, c)
            add_bias2(0, c)
        leaky1(3)
        quantise_h(2)
        quantise_h(3)
        def keep_clock2(c):
            for m in range(2):
                nc.tensor.matmul(
                    out=unread_ps[:, P * m : P * (m + 1)], lhsT=h2[:, c, HALF : HALF + P],
                    rhs=h2[:, c, ROWS - P : ROWS], start=True, stop=True,
                )

        for c in range(FEAT_TILES - 1):
            multiply2(1, c)
        leaky2(0, 0)
        multiply2(1, FEAT_TILES - 1)

        stages = (
            (lambda c: add_bias2(1, c), -3),
            (squares, 2),
            (inverse_deviation, 3),
            (lambda c: leaky2(0, c) if c else None, -5),
            (lambda c: leaky2(1, c), 0),
            (both_sums, 1),
            (keep_clock2, 1),
            (known, 2),
            (gain, 3),
            (normalise, 4),
            (store, 6),
        )
        for tick in range(-5, 2 * FEAT_TILES + 6):
            for stage, lag in stages:
                c, odd = divmod(tick - lag, 2)
                if not odd and 0 <= c < FEAT_TILES:
                    stage(c)
